import numpy as np
import ml_dtypes


def mxq(x, axis, fmt="e4m3"):
    dtype, down = {"e4m3": (ml_dtypes.float8_e4m3fn, 7), "e5m2": (ml_dtypes.float8_e5m2, 14)}[fmt]
    v = np.moveaxis(np.asarray(x, np.float32).astype(ml_dtypes.bfloat16).astype(np.float64), axis, -1)
    blocks = v.reshape(v.shape[:-1] + (-1, 32))
    amax = np.abs(blocks).max(-1, keepdims=True)
    byte = np.maximum(np.where(amax > 0, np.frexp(amax)[1] - 1 + 127, 0) - down, 1)
    scale = np.exp2(byte - 127.0)
    codes = (blocks / scale).astype(np.float32).astype(dtype).astype(np.float64)
    return np.moveaxis((codes * scale).reshape(v.shape), -1, axis)


WIDE = False


def mx_kscale(k):
    if not WIDE:
        return np.ones(k)
    levels = np.array([10, -10, 5, -5, 0])
    a = np.random.permutation(np.resize(levels, k // 512 * 4)).reshape(k // 512, 4)
    idx = np.arange(k)
    return np.exp2(a[idx // 512, idx % 128 // 32])


BF16 = ml_dtypes.bfloat16


def bf(x):
    return np.asarray(x, np.float32).astype(BF16)


def f64(x):
    return np.asarray(x).astype(np.float64)


N, B, T = 1024, 4, 512


def setup_inputs():
    s = mx_kscale(T)
    p = np.random.random(N)
    p = np.where(p < 0.05, 0.0, p)
    edge = np.random.random((N, N)) < p[None, :]
    return {"x": bf(np.random.standard_normal((B, T, N)) * 2.0 * s[None, :, None]),
            "edge_w": bf(edge * 0.4 * N * (0.5 + np.random.random((N, N)))),
            "weight": bf(np.random.standard_normal((T, T)) * 3.0 / np.sqrt(T) / s[:, None]),
            "bias": bf(np.random.standard_normal(T) * 0.1)}


def reference(x, edge_w, weight, bias):
    xp = f64(x).transpose(2, 0, 1)
    W = f64(edge_w)
    deg = W.sum(axis=0)
    dinv = np.where(deg > 0, np.where(deg > 0, deg, 1.0) ** -0.5, 0.0)
    Wn = dinv[:, None] * W * dinv[None, :]
    xw = mxq(xp, 2, "e4m3") @ mxq(f64(weight), 0, "e4m3")
    out = (mxq(Wn, 0, "e4m3").T @ mxq(xw.reshape(N, B * T), 0, "e4m3")).reshape(N, B, T) + f64(bias)
    return out.transpose(1, 2, 0)

@@ -1,0 +1,467 @@
+from contextlib import ExitStack
+
+import concourse.mybir as mybir
+from concourse.masks import make_identity
+
+F32 = mybir.dt.float32
+BF16 = mybir.dt.bfloat16
+U32 = mybir.dt.uint32
+U8 = mybir.dt.uint8
+FP8X4 = mybir.dt.float8_e4m3fn_x4
+ALU = mybir.AluOpType
+ACT = mybir.ActivationFunctionType
+
+P = 128
+PACK = 4
+B, T, N = 4, 512, 1024
+O = T
+NG = N // P
+NC = N // (P * PACK)
+NM = O // P
+NH = 2
+H = N // NH
+DEG_FLOOR = 2.0 ** -116
+
+FLOPS = 2 * N * B * T * O + 2 * N * N * B * O
+
+LOADS = ("w", "x0", "x1", "e0", "e1", "e2", "e3", "x2", "x3")
+
+PLAN = (
+    ("RWT",),
+    ("QWT",),
+    ("RX", 0, 0, "V"),
+    ("RX", 0, 1, "S"),
+    ("QX", 0, 0),
+    ("M1", 0, 0, 0),
+    ("RX", 1, 0, "V"),
+    ("RX", 1, 1, "S"),
+    ("M1", 0, 0, 1),
+    ("M1", 0, 0, 2),
+    ("M1", 0, 0, 3),
+    ("DG", 0),
+    ("QX", 0, 1),
+    ("DG", 1),
+    ("QX", 1, 0),
+    ("E1", 0, 0, 0, "S"),
+    ("DG", 2),
+    ("E1", 0, 0, 1, "V"),
+    ("E1", 0, 0, 2, "S"),
+    ("DG", 3),
+    ("QX", 1, 1),
+    ("BIAS",),
+    ("E1", 0, 0, 3, "S"),
+    ("DG", 4),
+    ("DG", 5),
+    ("QY", 0, 0),
+    ("DG", 6),
+    ("DG", 7),
+    ("M1", 1, 0, 0),
+    ("C1",),
+    ("C2",),
+    ("M1", 1, 0, 1),
+    ("E1", 1, 0, 0, "S"),
+    ("C3",),
+    ("M1", 1, 0, 2),
+    ("C4",),
+    ("E1", 1, 0, 1, "V"),
+    ("BT", 1),
+    ("RX", 2, 0, "S"),
+    ("M1", 1, 0, 3),
+    ("RX", 2, 1, "V"),
+    ("M1", 1, 1, 0),
+    ("M1", 1, 1, 1),
+    ("BT", 0),
+    ("CD", 1, "V"),
+    ("QX", 2, 1),
+    ("E1", 1, 0, 2, "S"),
+    ("SW", 1, 0, 0, "V"),
+    ("E1", 1, 0, 3, "S"),
+    ("M1", 2, 1, 0),
+    ("SW", 1, 0, 1, "V"),
+    ("E1", 2, 1, 0, "S"),
+    ("M1", 2, 1, 1),
+    ("SW", 1, 0, 2, "V"),
+    ("E1", 2, 1, 1, "S"),
+    ("M1", 2, 1, 2),
+    ("SW", 1, 0, 3, "V"),
+    ("E1", 2, 1, 2, "S"),
+    ("M1", 2, 1, 3),
+    ("SW", 1, 1, 0, "V"),
+    ("E1", 2, 1, 3, "S"),
+    ("M1", 1, 1, 2),
+    ("SW", 1, 1, 1, "V"),
+    ("E1", 1, 1, 0, "S"),
+    ("M1", 1, 1, 3),
+    ("SW", 1, 1, 2, "V"),
+    ("E1", 1, 1, 1, "S"),
+    ("M1", 0, 1, 0),
+    ("SW", 1, 1, 3, "V"),
+    ("E1", 1, 1, 2, "S"),
+    ("M1", 0, 1, 1),
+    ("E1", 1, 1, 3, "S"),
+    ("RW", 1, 0, "B"),
+    ("M1", 0, 1, 2),
+    ("CD", 0, "S"),
+    ("M1", 0, 1, 3),
+    ("RW", 1, 1, "B"),
+    ("SW", 0, 0, 0, "S"),
+    ("SW", 0, 0, 1, "S"),
+    ("QX", 2, 0),
+    ("SW", 0, 0, 2, "S"),
+    ("SW", 0, 0, 3, "S"),
+    ("QW", 1, 0),
+    ("E1", 0, 1, 0, "S"),
+    ("QW", 1, 1),
+    ("E1", 0, 1, 1, "S"),
+    ("QY", 2, 1),
+    ("M1", 2, 0, 0),
+    ("E1", 2, 0, 0, "S"),
+    ("M1", 2, 0, 1),
+    ("QY", 1, 0),
+    ("E1", 2, 0, 1, "S"),
+    ("M1", 2, 0, 2),
+    ("QY", 1, 1),
+    ("E1", 2, 0, 2, "S"),
+    ("M1", 2, 0, 3),
+    ("SW", 0, 1, 0, "V"),
+    ("M2", 1, 0, 1),
+    ("E1", 2, 0, 3, "S"),
+    ("SW", 0, 1, 1, "V"),
+    ("M2", 1, 1, 1),
+    ("E2", 1, 0, 1, "S"),
+    ("SW", 0, 1, 2, "V"),
+    ("M2", 1, 2, 1),
+    ("E2", 1, 1, 1, "S"),
+    ("QY", 2, 0),
+    ("M2", 1, 3, 1),
+    ("E2", 1, 2, 1, "S"),
+    ("SW", 0, 1, 3, "V"),
+    ("M2", 2, 0, 1),
+    ("E2", 1, 3, 1, "S"),
+    ("RW", 0, 0, "A"),
+    ("M2", 2, 1, 1),
+    ("E1", 0, 1, 2, "S"),
+    ("M2", 2, 2, 1),
+    ("E1", 0, 1, 3, "S"),
+    ("M2", 2, 3, 1),
+    ("E2", 2, 0, 1, "S"),
+    ("E2", 2, 1, 1, "S"),
+    ("QY", 0, 1),
+    ("E2", 2, 2, 1, "S"),
+    ("RW", 0, 1, "B"),
+    ("M2", 0, 0, 1),
+    ("E2", 2, 3, 1, "S"),
+    ("M2", 0, 1, 1),
+    ("E2", 0, 0, 1, "S"),
+    ("QW", 0, 0),
+    ("M2", 0, 2, 1),
+    ("E2", 0, 1, 1, "S"),
+    ("QW", 0, 1),
+    ("M2", 0, 3, 1),
+    ("E2", 0, 2, 1, "S"),
+    ("RX", 3, 0, "V"),
+    ("M2", 1, 0, 0),
+    ("E2", 0, 3, 1, "S"),
+    ("M2", 1, 1, 0),
+    ("E2", 1, 0, 0, "S"),
+    ("RX", 3, 1, "V"),
+    ("M2", 1, 2, 0),
+    ("E2", 1, 1, 0, "S"),
+    ("M2", 1, 3, 0),
+    ("E2", 1, 2, 0, "V"),
+    ("M2", 0, 0, 0),
+    ("E2", 1, 3, 0, "S"),
+    ("QX", 3, 0),
+    ("M2", 0, 1, 0),
+    ("E2", 0, 0, 0, "S"),
+    ("M2", 0, 2, 0),
+    ("QX", 3, 1),
+    ("E2", 0, 1, 0, "S"),
+    ("M1", 3, 0, 0),
+    ("E2", 0, 2, 0, "V"),
+    ("M1", 3, 0, 1),
+    ("E1", 3, 0, 0, "S"),
+    ("M1", 3, 0, 2),
+    ("E1", 3, 0, 1, "V"),
+    ("M1", 3, 0, 3),
+    ("E1", 3, 0, 2, "S"),
+    ("M1", 3, 1, 0),
+    ("E1", 3, 0, 3, "V"),
+    ("M1", 3, 1, 1),
+    ("E1", 3, 1, 0, "S"),
+    ("M1", 3, 1, 2),
+    ("E1", 3, 1, 1, "V"),
+    ("M1", 3, 1, 3),
+    ("E1", 3, 1, 2, "S"),
+    ("M2", 0, 3, 0),
+    ("QY", 3, 0),
+    ("E1", 3, 1, 3, "S"),
+    ("M2", 2, 0, 0),
+    ("E2", 0, 3, 0, "V"),
+    ("M2", 2, 1, 0),
+    ("E2", 2, 0, 0, "S"),
+    ("QY", 3, 1),
+    ("M2", 2, 2, 0),
+    ("E2", 2, 1, 0, "S"),
+    ("M2", 3, 0, 1),
+    ("E2", 2, 2, 0, "V"),
+    ("M2", 3, 1, 1),
+    ("E2", 3, 0, 1, "S"),
+    ("M2", 3, 2, 1),
+    ("E2", 3, 1, 1, "V"),
+    ("M2", 3, 3, 1),
+    ("E2", 3, 2, 1, "S"),
+    ("M2", 2, 3, 0),
+    ("E2", 3, 3, 1, "V"),
+    ("M2", 3, 0, 0),
+    ("E2", 2, 3, 0, "S"),
+    ("M2", 3, 1, 0),
+    ("E2", 3, 0, 0, "V"),
+    ("M2", 3, 2, 0),
+    ("E2", 3, 1, 0, "S"),
+    ("M2", 3, 3, 0),
+    ("E2", 3, 2, 0, "V"),
+    ("E2", 3, 3, 0, "S"),
+)
+
+
+def tile_graphembedding_pa_kernel(tc, x, edge_w, weight, bias, out):
+    nc = tc.nc
+    with ExitStack() as ctx:
+        const = ctx.enter_context(tc.tile_pool(name="const", bufs=1))
+        keep = ctx.enter_context(tc.tile_pool(name="keep", bufs=1))
+        xgp = ctx.enter_context(tc.tile_pool(name="xgp", bufs=2))
+        xwgp = ctx.enter_context(tc.tile_pool(name="xwgp", bufs=6))
+        plp = ctx.enter_context(tc.tile_pool(name="plp", bufs=2))
+        t1p = ctx.enter_context(tc.tile_pool(name="t1p", bufs=2))
+        wngp = ctx.enter_context(tc.tile_pool(name="wngp", bufs=2))
+        ostp = ctx.enter_context(tc.tile_pool(name="ostp", bufs=8))
+        ps1 = ctx.enter_context(tc.psum_pool(name="ps1", bufs=4))
+        ps2 = ctx.enter_context(tc.psum_pool(name="ps2", bufs=4))
+        ctx.enter_context(tc.manual_schedule())
+
+        one_col = const.tile([P, 1], F32, name="one_col")
+        nc.vector.memset(one_col[:], 1.0)
+        warm = const.tile([P, 1], F32, name="warm")
+        nc.scalar.activation(out=warm[:], in_=one_col[:], func=ACT.Sqrt)
+        ident = const.tile([P, P], F32, name="ident")
+        make_identity(nc, ident[:])
+        sel = const.tile([P, NG, P], BF16, name="sel")
+        nc.vector.memset(sel[:], 0.0)
+        for g in range(NG):
+            nc.vector.memset(sel[:, g, g : g + 1], 1.0)
+        bias_bf = const.tile([P, P], BF16, name="bias_bf")
+        nc.vector.memset(bias_bf[:], 0.0)
+        nc.scalar.dma_start(out=bias_bf[0:NM, :], in_=bias.rearrange("(m p) -> m p", p=P))
+
+        w_raw = keep.tile([P, PACK, O], BF16, name="w_raw")
+        x_raw = [keep.tile([P, PACK, N], BF16, name="x_raw%d" % b) for b in range(B)]
+        e_raw = keep.tile([P, NG, N], BF16, name="e_raw")
+        e_view = edge_w.rearrange("(g p) d -> p g d", p=P)
+        for what in LOADS:
+            if what == "w":
+                nc.sync.dma_start(out=w_raw[:], in_=weight.rearrange("(p j) o -> p j o", j=PACK))
+            for b in range(B):
+                if what == "x%d" % b:
+                    nc.sync.dma_start(out=x_raw[b][:], in_=x[b].rearrange("(p j) s -> p j s", j=PACK))
+                if what == "e%d" % b:
+                    nc.sync.dma_start(out=e_raw[:, 2 * b : 2 * b + 2, :], in_=e_view[:, 2 * b : 2 * b + 2, :])
+
+        bias_f = const.tile([P, P], F32, name="bias_f")
+        bias_col = const.tile([P, NM], F32, name="bias_col")
+
+        wg = keep.tile([P, O, PACK], BF16, name="wg", align_bytes=64)
+        wc = keep.tile([P, O], U32, name="wc", align_bytes=64)
+        ws = keep.tile([P, O], U8, name="ws", align_bytes=64)
+        xc = [keep.tile([P, N], U32, name="xc%d" % b, align_bytes=64) for b in range(B)]
+        xs = [keep.tile([P, N], U8, name="xs%d" % b, align_bytes=64) for b in range(B)]
+        xwc = [keep.tile([P, NC, O], U32, name="xwc%d" % b, align_bytes=64) for b in range(B)]
+        xws = [keep.tile([P, NC, O], U8, name="xws%d" % b, align_bytes=64) for b in range(B)]
+        wnc = keep.tile([P, NC, N], U32, name="wnc", align_bytes=64)
+        wns = keep.tile([P, NC, N], U8, name="wns", align_bytes=64)
+        dinv = const.tile([P, NG], F32, name="dinv")
+        dm = const.tile([P, NG], F32, name="dm")
+        sq = const.tile([P, NG], F32, name="sq")
+        rc = const.tile([P, NG], F32, name="rc")
+        dd = keep.tile([P, N], F32, name="dd")
+        live = {}
+
+        def regroup(engine, dst, src):
+            dst4 = dst.rearrange("p (c i) t -> p c t i", i=4)
+            src4 = src.rearrange("p t (c i) -> p c t i", i=4)
+            if engine == "V":
+                nc.vector.tensor_copy(out=dst4, in_=src4)
+            else:
+                nc.scalar.copy(out=dst4, in_=src4)
+
+        for step in PLAN:
+            kind = step[0]
+            if kind == "BIAS":
+                nc.vector.tensor_copy(out=bias_f[:], in_=bias_bf[:])
+                bias_ps = ps2.tile([P, P], F32, name="bias_ps", tag="m2")
+                nc.tensor.transpose(bias_ps[:], bias_f[:], ident[:])
+                nc.vector.tensor_copy(out=bias_col[:], in_=bias_ps[:, 0:NM])
+            elif kind == "RWT":
+                regroup("V", wg[:], w_raw[:])
+            elif kind == "QWT":
+                nc.vector.quantize_mx(
+                    out=wc[:].bitcast(FP8X4), scales=ws[:], in_=wg[:].rearrange("p o j -> p (o j)")
+                )
+            elif kind == "RX":
+                b, h = step[1], step[2]
+                if ("xg", b) not in live:
+                    live[("xg", b)] = xgp.tile([P, N, PACK], BF16, name="xg", tag="xg", align_bytes=64)
+                regroup(step[3], live[("xg", b)][:, h * H : (h + 1) * H, :], x_raw[b][:, :, h * H : (h + 1) * H])
+            elif kind == "QX":
+                b, h = step[1], step[2]
+                nc.vector.quantize_mx(
+                    out=xc[b][:, h * H : (h + 1) * H].bitcast(FP8X4),
+                    scales=xs[b][:, h * H : (h + 1) * H],
+                    in_=live[("xg", b)][:, h * H : (h + 1) * H, :].rearrange("p s j -> p (s j)"),
+                )
+            elif kind == "DG":
+                k = step[1]
+                if k == 0:
+                    live["deg"] = ps2.tile([P, P], F32, name="deg_ps", tag="m2")
+                for g in range(NG):
+                    nc.tensor.matmul(
+                        live["deg"][:],
+                        lhsT=e_raw[:, k, g * P : (g + 1) * P],
+                        rhs=sel[:, g, :],
+                        start=(k == 0 and g == 0),
+                        stop=(k == NG - 1 and g == NG - 1),
+                    )
+            elif kind == "C1":
+                nc.vector.tensor_scalar(
+                    out=dm[:], in0=live["deg"][:, 0:NG], scalar1=DEG_FLOOR, scalar2=None, op0=ALU.max
+                )
+            elif kind == "C2":
+                nc.scalar.activation(out=sq[:], in_=dm[:], func=ACT.Sqrt)
+            elif kind == "C3":
+                nc.vector.reciprocal(out=rc[:], in_=sq[:])
+            elif kind == "C4":
+                nc.vector.scalar_tensor_tensor(
+                    out=dinv[:], in0=live["deg"][:, 0:NG], scalar=0.0, in1=rc[:], op0=ALU.is_gt, op1=ALU.mult
+                )
+            elif kind == "BT":
+                h = step[1]
+                live[("dd", h)] = ps2.tile([P, H], F32, name="dd_ps", tag="m2")
+                for q in range(4):
+                    g = h * 4 + q
+                    nc.tensor.transpose(
+                        live[("dd", h)][:, q * P : (q + 1) * P], dinv[:, g : g + 1].to_broadcast([P, P]), ident[:]
+                    )
+            elif kind == "CD":
+                h = step[1]
+                if step[2] == "V":
+                    nc.vector.tensor_copy(out=dd[:, h * H : (h + 1) * H], in_=live[("dd", h)][:])
+                else:
+                    nc.scalar.copy(out=dd[:, h * H : (h + 1) * H], in_=live[("dd", h)][:])
+            elif kind == "SW":
+                h, c, j = step[1], step[2], step[3]
+                g = c * PACK + j
+                if step[4] == "V":
+                    if j == 0:
+                        live[("pl", h, c)] = plp.tile([P, PACK, H], BF16, name="wn_pl", tag="wn_pl")
+                    nc.vector.scalar_tensor_tensor(
+                        out=live[("pl", h, c)][:, j, :],
+                        in0=e_raw[:, g, h * H : (h + 1) * H],
+                        scalar=dinv[:, g : g + 1],
+                        in1=dd[:, h * H : (h + 1) * H],
+                        op0=ALU.mult,
+                        op1=ALU.mult,
+                    )
+                else:
+                    if j == 0:
+                        live[("pl", h, c)] = t1p.tile([P, PACK, H], F32, name="wn_t1", tag="wn_t1")
+                    nc.scalar.activation(
+                        out=live[("pl", h, c)][:, j, :],
+                        in_=e_raw[:, g, h * H : (h + 1) * H],
+                        func=ACT.Copy,
+                        scale=dinv[:, g : g + 1],
+                    )
+            elif kind == "RW":
+                h, c = step[1], step[2]
+                live[("wng", h, c)] = wngp.tile([P, H, PACK], BF16, name="wng", tag="wng", align_bytes=64)
+                if step[3] == "B":
+                    regroup("V", live[("wng", h, c)][:], live[("pl", h, c)][:])
+                else:
+                    nc.vector.tensor_tensor(
+                        out=live[("wng", h, c)][:],
+                        in0=live[("pl", h, c)][:].rearrange("p j d -> p d j"),
+                        in1=dd[:, h * H : (h + 1) * H].unsqueeze(2).to_broadcast([P, H, PACK]),
+                        op=ALU.mult,
+                    )
+            elif kind == "QW":
+                h, c = step[1], step[2]
+                nc.vector.quantize_mx(
+                    out=wnc[:, c, h * H : (h + 1) * H].bitcast(FP8X4),
+                    scales=wns[:, c, h * H : (h + 1) * H],
+                    in_=live[("wng", h, c)][:].rearrange("p d j -> p (d j)"),
+                )
+            elif kind == "M1":
+                b, c, ob = step[1], step[2], step[3]
+                bank = ps1.tile([P, PACK, P], F32, name="bank1", tag="m1")
+                live[("m1", b, c, ob)] = bank
+                for j in range(PACK):
+                    g = c * PACK + j
+                    nc.tensor.matmul_mx(
+                        out=bank[:, j, :],
+                        lhsT=xc[b][:, g * P : (g + 1) * P].bitcast(FP8X4),
+                        lhsT_scale=xs[b][:, g * P : (g + 1) * P],
+                        rhs=wc[:, ob * P : (ob + 1) * P].bitcast(FP8X4),
+                        rhs_scale=ws[:, ob * P : (ob + 1) * P],
+                        start=True,
+                        stop=True,
+                    )
+            elif kind == "E1":
+                b, c, ob = step[1], step[2], step[3]
+                if ("xwg", b, c) not in live:
+                    live[("xwg", b, c)] = xwgp.tile([P, O, PACK], BF16, name="xwg", tag="xwg", align_bytes=64)
+                dst = live[("xwg", b, c)][:, ob * P : (ob + 1) * P, :]
+                src = live[("m1", b, c, ob)][:].rearrange("p j o -> p o j")
+                if step[4] == "V":
+                    nc.vector.tensor_copy(out=dst, in_=src)
+                else:
+                    nc.scalar.copy(out=dst, in_=src)
+            elif kind == "QY":
+                b, c = step[1], step[2]
+                nc.vector.quantize_mx(
+                    out=xwc[b][:, c, :].bitcast(FP8X4),
+                    scales=xws[b][:, c, :],
+                    in_=live[("xwg", b, c)][:].rearrange("p o j -> p (o j)"),
+                )
+            elif kind == "M2":
+                b, m, h = step[1], step[2], step[3]
+                acc = ps2.tile([P, H], F32, name="acc", tag="m2")
+                live[("m2", b, m, h)] = acc
+                for c in range(NC):
+                    nc.tensor.matmul_mx(
+                        out=acc[:],
+                        lhsT=xwc[b][:, c, m * P : (m + 1) * P].bitcast(FP8X4),
+                        lhsT_scale=xws[b][:, c, m * P : (m + 1) * P],
+                        rhs=wnc[:, c, h * H : (h + 1) * H].bitcast(FP8X4),
+                        rhs_scale=wns[:, c, h * H : (h + 1) * H],
+                        start=(c == 0),
+                        stop=(c == NC - 1),
+                    )
+            elif kind == "E2":
+                b, m, h = step[1], step[2], step[3]
+                ost = ostp.tile([P, H], F32, name="ost", tag="ost")
+                if step[4] == "V":
+                    nc.vector.tensor_scalar(
+                        out=ost[:],
+                        in0=live[("m2", b, m, h)][:],
+                        scalar1=bias_col[:, m : m + 1],
+                        scalar2=None,
+                        op0=ALU.add,
+                    )
+                else:
+                    nc.scalar.activation(
+                        out=ost[:],
+                        in_=live[("m2", b, m, h)][:],
+                        func=ACT.Identity,
+                        bias=bias_col[:, m : m + 1],
+                        scale=1.0,
+                    )
+                nc.sync.dma_start(out=out[b, m * P : (m + 1) * P, h * H : (h + 1) * H], in_=ost[:])

@@ -15,214 +15,14 @@ P = 128
 PACK = 4
 B, T, N = 4, 512, 1024
 O = T
-NG = N // P
-NC = N // (P * PACK)
-NM = O // P
-NH = 2
-H = N // NH
+TILES = N // P
+PASSES = N // (P * PACK)
+BLOCKS = O // P
+HALVES = 2
+H = N // HALVES
 DEG_FLOOR = 2.0 ** -116
 
 FLOPS = 2 * N * B * T * O + 2 * N * N * B * O
-
-LOADS = ("w", "x0", "x1", "e0", "e1", "e2", "e3", "x2", "x3")
-
-PLAN = (
-    ("RWT",),
-    ("QWT",),
-    ("RX", 0, 0, "V"),
-    ("RX", 0, 1, "S"),
-    ("QX", 0, 0),
-    ("M1", 0, 0, 0),
-    ("RX", 1, 0, "V"),
-    ("RX", 1, 1, "S"),
-    ("M1", 0, 0, 1),
-    ("M1", 0, 0, 2),
-    ("M1", 0, 0, 3),
-    ("DG", 0),
-    ("QX", 0, 1),
-    ("DG", 1),
-    ("QX", 1, 0),
-    ("E1", 0, 0, 0, "S"),
-    ("DG", 2),
-    ("E1", 0, 0, 1, "V"),
-    ("E1", 0, 0, 2, "S"),
-    ("DG", 3),
-    ("QX", 1, 1),
-    ("BIAS",),
-    ("E1", 0, 0, 3, "S"),
-    ("DG", 4),
-    ("DG", 5),
-    ("QY", 0, 0),
-    ("DG", 6),
-    ("DG", 7),
-    ("M1", 1, 0, 0),
-    ("C1",),
-    ("C2",),
-    ("M1", 1, 0, 1),
-    ("E1", 1, 0, 0, "S"),
-    ("C3",),
-    ("M1", 1, 0, 2),
-    ("C4",),
-    ("E1", 1, 0, 1, "V"),
-    ("BT", 1),
-    ("RX", 2, 0, "S"),
-    ("M1", 1, 0, 3),
-    ("RX", 2, 1, "V"),
-    ("M1", 1, 1, 0),
-    ("M1", 1, 1, 1),
-    ("BT", 0),
-    ("CD", 1, "V"),
-    ("QX", 2, 1),
-    ("E1", 1, 0, 2, "S"),
-    ("SW", 1, 0, 0, "V"),
-    ("E1", 1, 0, 3, "S"),
-    ("M1", 2, 1, 0),
-    ("SW", 1, 0, 1, "V"),
-    ("E1", 2, 1, 0, "S"),
-    ("M1", 2, 1, 1),
-    ("SW", 1, 0, 2, "V"),
-    ("E1", 2, 1, 1, "S"),
-    ("M1", 2, 1, 2),
-    ("SW", 1, 0, 3, "V"),
-    ("E1", 2, 1, 2, "S"),
-    ("M1", 2, 1, 3),
-    ("SW", 1, 1, 0, "V"),
-    ("E1", 2, 1, 3, "S"),
-    ("M1", 1, 1, 2),
-    ("SW", 1, 1, 1, "V"),
-    ("E1", 1, 1, 0, "S"),
-    ("M1", 1, 1, 3),
-    ("SW", 1, 1, 2, "V"),
-    ("E1", 1, 1, 1, "S"),
-    ("M1", 0, 1, 0),
-    ("SW", 1, 1, 3, "V"),
-    ("E1", 1, 1, 2, "S"),
-    ("M1", 0, 1, 1),
-    ("E1", 1, 1, 3, "S"),
-    ("RW", 1, 0, "B"),
-    ("M1", 0, 1, 2),
-    ("CD", 0, "S"),
-    ("M1", 0, 1, 3),
-    ("RW", 1, 1, "B"),
-    ("SW", 0, 0, 0, "S"),
-    ("SW", 0, 0, 1, "S"),
-    ("QX", 2, 0),
-    ("SW", 0, 0, 2, "S"),
-    ("SW", 0, 0, 3, "S"),
-    ("QW", 1, 0),
-    ("E1", 0, 1, 0, "S"),
-    ("QW", 1, 1),
-    ("E1", 0, 1, 1, "S"),
-    ("QY", 2, 1),
-    ("M1", 2, 0, 0),
-    ("E1", 2, 0, 0, "S"),
-    ("M1", 2, 0, 1),
-    ("QY", 1, 0),
-    ("E1", 2, 0, 1, "S"),
-    ("M1", 2, 0, 2),
-    ("QY", 1, 1),
-    ("E1", 2, 0, 2, "S"),
-    ("M1", 2, 0, 3),
-    ("SW", 0, 1, 0, "V"),
-    ("M2", 1, 0, 1),
-    ("E1", 2, 0, 3, "S"),
-    ("SW", 0, 1, 1, "V"),
-    ("M2", 1, 1, 1),
-    ("E2", 1, 0, 1, "S"),
-    ("SW", 0, 1, 2, "V"),
-    ("M2", 1, 2, 1),
-    ("E2", 1, 1, 1, "S"),
-    ("QY", 2, 0),
-    ("M2", 1, 3, 1),
-    ("E2", 1, 2, 1, "S"),
-    ("SW", 0, 1, 3, "V"),
-    ("M2", 2, 0, 1),
-    ("E2", 1, 3, 1, "S"),
-    ("RW", 0, 0, "A"),
-    ("M2", 2, 1, 1),
-    ("E1", 0, 1, 2, "S"),
-    ("M2", 2, 2, 1),
-    ("E1", 0, 1, 3, "S"),
-    ("M2", 2, 3, 1),
-    ("E2", 2, 0, 1, "S"),
-    ("E2", 2, 1, 1, "S"),
-    ("QY", 0, 1),
-    ("E2", 2, 2, 1, "S"),
-    ("RW", 0, 1, "B"),
-    ("M2", 0, 0, 1),
-    ("E2", 2, 3, 1, "S"),
-    ("M2", 0, 1, 1),
-    ("E2", 0, 0, 1, "S"),
-    ("QW", 0, 0),
-    ("M2", 0, 2, 1),
-    ("E2", 0, 1, 1, "S"),
-    ("QW", 0, 1),
-    ("M2", 0, 3, 1),
-    ("E2", 0, 2, 1, "S"),
-    ("RX", 3, 0, "V"),
-    ("M2", 1, 0, 0),
-    ("E2", 0, 3, 1, "S"),
-    ("M2", 1, 1, 0),
-    ("E2", 1, 0, 0, "S"),
-    ("RX", 3, 1, "V"),
-    ("M2", 1, 2, 0),
-    ("E2", 1, 1, 0, "S"),
-    ("M2", 1, 3, 0),
-    ("E2", 1, 2, 0, "V"),
-    ("M2", 0, 0, 0),
-    ("E2", 1, 3, 0, "S"),
-    ("QX", 3, 0),
-    ("M2", 0, 1, 0),
-    ("E2", 0, 0, 0, "S"),
-    ("M2", 0, 2, 0),
-    ("QX", 3, 1),
-    ("E2", 0, 1, 0, "S"),
-    ("M1", 3, 0, 0),
-    ("E2", 0, 2, 0, "V"),
-    ("M1", 3, 0, 1),
-    ("E1", 3, 0, 0, "S"),
-    ("M1", 3, 0, 2),
-    ("E1", 3, 0, 1, "V"),
-    ("M1", 3, 0, 3),
-    ("E1", 3, 0, 2, "S"),
-    ("M1", 3, 1, 0),
-    ("E1", 3, 0, 3, "V"),
-    ("M1", 3, 1, 1),
-    ("E1", 3, 1, 0, "S"),
-    ("M1", 3, 1, 2),
-    ("E1", 3, 1, 1, "V"),
-    ("M1", 3, 1, 3),
-    ("E1", 3, 1, 2, "S"),
-    ("M2", 0, 3, 0),
-    ("QY", 3, 0),
-    ("E1", 3, 1, 3, "S"),
-    ("M2", 2, 0, 0),
-    ("E2", 0, 3, 0, "V"),
-    ("M2", 2, 1, 0),
-    ("E2", 2, 0, 0, "S"),
-    ("QY", 3, 1),
-    ("M2", 2, 2, 0),
-    ("E2", 2, 1, 0, "S"),
-    ("M2", 3, 0, 1),
-    ("E2", 2, 2, 0, "V"),
-    ("M2", 3, 1, 1),
-    ("E2", 3, 0, 1, "S"),
-    ("M2", 3, 2, 1),
-    ("E2", 3, 1, 1, "V"),
-    ("M2", 3, 3, 1),
-    ("E2", 3, 2, 1, "S"),
-    ("M2", 2, 3, 0),
-    ("E2", 3, 3, 1, "V"),
-    ("M2", 3, 0, 0),
-    ("E2", 2, 3, 0, "S"),
-    ("M2", 3, 1, 0),
-    ("E2", 3, 0, 0, "V"),
-    ("M2", 3, 2, 0),
-    ("E2", 3, 1, 0, "S"),
-    ("M2", 3, 3, 0),
-    ("E2", 3, 2, 0, "V"),
-    ("E2", 3, 3, 0, "S"),
-)
 
 
 def tile_graphembedding_pa_kernel(tc, x, edge_w, weight, bias, out):
@@ -230,238 +30,278 @@ def tile_graphembedding_pa_kernel(tc, x, edge_w, weight, bias, out):
     with ExitStack() as ctx:
         const = ctx.enter_context(tc.tile_pool(name="const", bufs=1))
         keep = ctx.enter_context(tc.tile_pool(name="keep", bufs=1))
-        xgp = ctx.enter_context(tc.tile_pool(name="xgp", bufs=2))
-        xwgp = ctx.enter_context(tc.tile_pool(name="xwgp", bufs=6))
-        plp = ctx.enter_context(tc.tile_pool(name="plp", bufs=2))
-        t1p = ctx.enter_context(tc.tile_pool(name="t1p", bufs=2))
-        wngp = ctx.enter_context(tc.tile_pool(name="wngp", bufs=2))
-        ostp = ctx.enter_context(tc.tile_pool(name="ostp", bufs=8))
-        ps1 = ctx.enter_context(tc.psum_pool(name="ps1", bufs=4))
-        ps2 = ctx.enter_context(tc.psum_pool(name="ps2", bufs=4))
+        x_pool = ctx.enter_context(tc.tile_pool(name="x_pool", bufs=2))
+        xw_pool = ctx.enter_context(tc.tile_pool(name="xw_pool", bufs=6))
+        wn_pool = ctx.enter_context(tc.tile_pool(name="wn_pool", bufs=2))
+        out_pool = ctx.enter_context(tc.tile_pool(name="out_pool", bufs=8))
+        psum_xw = ctx.enter_context(tc.psum_pool(name="psum_xw", bufs=4))
+        psum_out = ctx.enter_context(tc.psum_pool(name="psum_out", bufs=4))
         ctx.enter_context(tc.manual_schedule())
+
+        bias_rows = const.tile([P, P], BF16, name="bias_rows")
+        nc.gpsimd.memset(bias_rows[:], 0.0)
+        nc.gpsimd.dma_start(out=bias_rows[0:BLOCKS, :], in_=bias.rearrange("(m p) -> m p", p=P))
+        ident_bf = const.tile([P, P], BF16, name="ident_bf")
+        make_identity(nc, ident_bf[:])
+        ident = const.tile([P, P], F32, name="ident")
+        make_identity(nc, ident[:])
 
         one_col = const.tile([P, 1], F32, name="one_col")
         nc.vector.memset(one_col[:], 1.0)
         warm = const.tile([P, 1], F32, name="warm")
         nc.scalar.activation(out=warm[:], in_=one_col[:], func=ACT.Sqrt)
-        ident = const.tile([P, P], F32, name="ident")
-        make_identity(nc, ident[:])
-        sel = const.tile([P, NG, P], BF16, name="sel")
-        nc.vector.memset(sel[:], 0.0)
-        for g in range(NG):
-            nc.vector.memset(sel[:, g, g : g + 1], 1.0)
-        bias_bf = const.tile([P, P], BF16, name="bias_bf")
-        nc.vector.memset(bias_bf[:], 0.0)
-        nc.scalar.dma_start(out=bias_bf[0:NM, :], in_=bias.rearrange("(m p) -> m p", p=P))
+        select = const.tile([P, TILES, P], BF16, name="select")
+        nc.vector.memset(select[:], 0.0)
+        for g in range(TILES):
+            nc.vector.memset(select[:, g, g : g + 1], 1.0)
 
         w_raw = keep.tile([P, PACK, O], BF16, name="w_raw")
         x_raw = [keep.tile([P, PACK, N], BF16, name="x_raw%d" % b) for b in range(B)]
-        e_raw = keep.tile([P, NG, N], BF16, name="e_raw")
+        e_raw = keep.tile([P, TILES, N], BF16, name="e_raw")
         e_view = edge_w.rearrange("(g p) d -> p g d", p=P)
-        for what in LOADS:
-            if what == "w":
-                nc.sync.dma_start(out=w_raw[:], in_=weight.rearrange("(p j) o -> p j o", j=PACK))
-            for b in range(B):
-                if what == "x%d" % b:
-                    nc.sync.dma_start(out=x_raw[b][:], in_=x[b].rearrange("(p j) s -> p j s", j=PACK))
-                if what == "e%d" % b:
-                    nc.sync.dma_start(out=e_raw[:, 2 * b : 2 * b + 2, :], in_=e_view[:, 2 * b : 2 * b + 2, :])
 
-        bias_f = const.tile([P, P], F32, name="bias_f")
-        bias_col = const.tile([P, NM], F32, name="bias_col")
+        def load_x(b):
+            nc.sync.dma_start(out=x_raw[b][:], in_=x[b].rearrange("(p j) s -> p j s", j=PACK))
 
-        wg = keep.tile([P, O, PACK], BF16, name="wg", align_bytes=64)
-        wc = keep.tile([P, O], U32, name="wc", align_bytes=64)
-        ws = keep.tile([P, O], U8, name="ws", align_bytes=64)
-        xc = [keep.tile([P, N], U32, name="xc%d" % b, align_bytes=64) for b in range(B)]
-        xs = [keep.tile([P, N], U8, name="xs%d" % b, align_bytes=64) for b in range(B)]
-        xwc = [keep.tile([P, NC, O], U32, name="xwc%d" % b, align_bytes=64) for b in range(B)]
-        xws = [keep.tile([P, NC, O], U8, name="xws%d" % b, align_bytes=64) for b in range(B)]
-        wnc = keep.tile([P, NC, N], U32, name="wnc", align_bytes=64)
-        wns = keep.tile([P, NC, N], U8, name="wns", align_bytes=64)
-        dinv = const.tile([P, NG], F32, name="dinv")
-        dm = const.tile([P, NG], F32, name="dm")
-        sq = const.tile([P, NG], F32, name="sq")
-        rc = const.tile([P, NG], F32, name="rc")
-        dd = keep.tile([P, N], F32, name="dd")
+        nc.sync.dma_start(out=w_raw[:], in_=weight.rearrange("(p j) o -> p j o", j=PACK))
+        load_x(0)
+        load_x(1)
+        load_x(2)
+        for g in range(0, TILES, 2):
+            nc.sync.dma_start(out=e_raw[:, g : g + 2, :], in_=e_view[:, g : g + 2, :])
+        load_x(3)
+
+        w_grouped = keep.tile([P, O, PACK], BF16, name="w_grouped", align_bytes=64)
+        w_codes = keep.tile([P, O], U32, name="w_codes", align_bytes=64)
+        w_scales = keep.tile([P, O], U8, name="w_scales", align_bytes=64)
+        x_codes = [keep.tile([P, N], U32, name="x_codes%d" % b, align_bytes=64) for b in range(B)]
+        x_scales = [keep.tile([P, N], U8, name="x_scales%d" % b, align_bytes=64) for b in range(B)]
+        xw_codes = [keep.tile([P, PASSES, O], U32, name="xw_codes%d" % b, align_bytes=64) for b in range(B)]
+        xw_scales = [keep.tile([P, PASSES, O], U8, name="xw_scales%d" % b, align_bytes=64) for b in range(B)]
+        wn_codes = keep.tile([P, PASSES, N], U32, name="wn_codes", align_bytes=64)
+        wn_scales = keep.tile([P, PASSES, N], U8, name="wn_scales", align_bytes=64)
+        bias_col = const.tile([P, BLOCKS], F32, name="bias_col")
+        deg_floor = const.tile([P, TILES], F32, name="deg_floor")
+        deg_sqrt = const.tile([P, TILES], F32, name="deg_sqrt")
+        deg_rsqrt = const.tile([P, TILES], F32, name="deg_rsqrt")
+        dinv_col = const.tile([P, TILES], F32, name="dinv_col")
+        dinv_row = keep.tile([P, N], F32, name="dinv_row")
         live = {}
 
-        def regroup(engine, dst, src):
-            dst4 = dst.rearrange("p (c i) t -> p c t i", i=4)
-            src4 = src.rearrange("p t (c i) -> p c t i", i=4)
-            if engine == "V":
-                nc.vector.tensor_copy(out=dst4, in_=src4)
-            else:
-                nc.scalar.copy(out=dst4, in_=src4)
+        def half(h):
+            return slice(h * H, (h + 1) * H)
 
-        for step in PLAN:
-            kind = step[0]
-            if kind == "BIAS":
-                nc.vector.tensor_copy(out=bias_f[:], in_=bias_bf[:])
-                bias_ps = ps2.tile([P, P], F32, name="bias_ps", tag="m2")
-                nc.tensor.transpose(bias_ps[:], bias_f[:], ident[:])
-                nc.vector.tensor_copy(out=bias_col[:], in_=bias_ps[:, 0:NM])
-            elif kind == "RWT":
-                regroup("V", wg[:], w_raw[:])
-            elif kind == "QWT":
-                nc.vector.quantize_mx(
-                    out=wc[:].bitcast(FP8X4), scales=ws[:], in_=wg[:].rearrange("p o j -> p (o j)")
-                )
-            elif kind == "RX":
-                b, h = step[1], step[2]
-                if ("xg", b) not in live:
-                    live[("xg", b)] = xgp.tile([P, N, PACK], BF16, name="xg", tag="xg", align_bytes=64)
-                regroup(step[3], live[("xg", b)][:, h * H : (h + 1) * H, :], x_raw[b][:, :, h * H : (h + 1) * H])
-            elif kind == "QX":
-                b, h = step[1], step[2]
-                nc.vector.quantize_mx(
-                    out=xc[b][:, h * H : (h + 1) * H].bitcast(FP8X4),
-                    scales=xs[b][:, h * H : (h + 1) * H],
-                    in_=live[("xg", b)][:, h * H : (h + 1) * H, :].rearrange("p s j -> p (s j)"),
-                )
-            elif kind == "DG":
-                k = step[1]
-                if k == 0:
-                    live["deg"] = ps2.tile([P, P], F32, name="deg_ps", tag="m2")
-                for g in range(NG):
-                    nc.tensor.matmul(
-                        live["deg"][:],
-                        lhsT=e_raw[:, k, g * P : (g + 1) * P],
-                        rhs=sel[:, g, :],
-                        start=(k == 0 and g == 0),
-                        stop=(k == NG - 1 and g == NG - 1),
-                    )
-            elif kind == "C1":
-                nc.vector.tensor_scalar(
-                    out=dm[:], in0=live["deg"][:, 0:NG], scalar1=DEG_FLOOR, scalar2=None, op0=ALU.max
-                )
-            elif kind == "C2":
-                nc.scalar.activation(out=sq[:], in_=dm[:], func=ACT.Sqrt)
-            elif kind == "C3":
-                nc.vector.reciprocal(out=rc[:], in_=sq[:])
-            elif kind == "C4":
-                nc.vector.scalar_tensor_tensor(
-                    out=dinv[:], in0=live["deg"][:, 0:NG], scalar=0.0, in1=rc[:], op0=ALU.is_gt, op1=ALU.mult
-                )
-            elif kind == "BT":
-                h = step[1]
-                live[("dd", h)] = ps2.tile([P, H], F32, name="dd_ps", tag="m2")
-                for q in range(4):
-                    g = h * 4 + q
-                    nc.tensor.transpose(
-                        live[("dd", h)][:, q * P : (q + 1) * P], dinv[:, g : g + 1].to_broadcast([P, P]), ident[:]
-                    )
-            elif kind == "CD":
-                h = step[1]
-                if step[2] == "V":
-                    nc.vector.tensor_copy(out=dd[:, h * H : (h + 1) * H], in_=live[("dd", h)][:])
-                else:
-                    nc.scalar.copy(out=dd[:, h * H : (h + 1) * H], in_=live[("dd", h)][:])
-            elif kind == "SW":
-                h, c, j = step[1], step[2], step[3]
-                g = c * PACK + j
-                if step[4] == "V":
-                    if j == 0:
-                        live[("pl", h, c)] = plp.tile([P, PACK, H], BF16, name="wn_pl", tag="wn_pl")
-                    nc.vector.scalar_tensor_tensor(
-                        out=live[("pl", h, c)][:, j, :],
-                        in0=e_raw[:, g, h * H : (h + 1) * H],
-                        scalar=dinv[:, g : g + 1],
-                        in1=dd[:, h * H : (h + 1) * H],
-                        op0=ALU.mult,
-                        op1=ALU.mult,
-                    )
-                else:
-                    if j == 0:
-                        live[("pl", h, c)] = t1p.tile([P, PACK, H], F32, name="wn_t1", tag="wn_t1")
-                    nc.scalar.activation(
-                        out=live[("pl", h, c)][:, j, :],
-                        in_=e_raw[:, g, h * H : (h + 1) * H],
-                        func=ACT.Copy,
-                        scale=dinv[:, g : g + 1],
-                    )
-            elif kind == "RW":
-                h, c = step[1], step[2]
-                live[("wng", h, c)] = wngp.tile([P, H, PACK], BF16, name="wng", tag="wng", align_bytes=64)
-                if step[3] == "B":
-                    regroup("V", live[("wng", h, c)][:], live[("pl", h, c)][:])
-                else:
-                    nc.vector.tensor_tensor(
-                        out=live[("wng", h, c)][:],
-                        in0=live[("pl", h, c)][:].rearrange("p j d -> p d j"),
-                        in1=dd[:, h * H : (h + 1) * H].unsqueeze(2).to_broadcast([P, H, PACK]),
-                        op=ALU.mult,
-                    )
-            elif kind == "QW":
-                h, c = step[1], step[2]
-                nc.vector.quantize_mx(
-                    out=wnc[:, c, h * H : (h + 1) * H].bitcast(FP8X4),
-                    scales=wns[:, c, h * H : (h + 1) * H],
-                    in_=live[("wng", h, c)][:].rearrange("p d j -> p (d j)"),
-                )
-            elif kind == "M1":
-                b, c, ob = step[1], step[2], step[3]
-                bank = ps1.tile([P, PACK, P], F32, name="bank1", tag="m1")
-                live[("m1", b, c, ob)] = bank
+        def block(i):
+            return slice(i * P, (i + 1) * P)
+
+        def copy(engine, dst, src):
+            if engine == "V":
+                nc.vector.tensor_copy(out=dst, in_=src)
+            else:
+                nc.scalar.copy(out=dst, in_=src)
+
+        def regroup(engine, dst, src):
+            copy(
+                engine,
+                dst.rearrange("p (c i) t -> p c t i", i=4),
+                src.rearrange("p t (c i) -> p c t i", i=4),
+            )
+
+        def quantise(codes, scales, grouped):
+            nc.vector.quantize_mx(
+                out=codes.bitcast(FP8X4), scales=scales, in_=grouped.rearrange("p w j -> p (w j)")
+            )
+
+        def bias_transpose():
+            live["bias"] = psum_out.tile([P, P], BF16, name="bias_ps", tag="bank")
+            nc.tensor.transpose(live["bias"][:], bias_rows[:], ident_bf[:])
+
+        def bias_copy():
+            nc.vector.tensor_copy(out=bias_col[:], in_=live["bias"][:, 0:BLOCKS])
+
+        def weight_quantise():
+            regroup("V", w_grouped[:], w_raw[:])
+            quantise(w_codes[:], w_scales[:], w_grouped[:])
+
+        def x_regroup(b, h, engine):
+            if h == 0:
+                live["x", b] = x_pool.tile([P, N, PACK], BF16, name="x_grouped", tag="x_grouped", align_bytes=64)
+            regroup(engine, live["x", b][:, half(h), :], x_raw[b][:, :, half(h)])
+
+        def x_quantise(b, h):
+            quantise(x_codes[b][:, half(h)], x_scales[b][:, half(h)], live["x", b][:, half(h), :])
+
+        def first_matmul(b, c, engines):
+            grouped = xw_pool.tile([P, O, PACK], BF16, name="xw_grouped", tag="xw_grouped", align_bytes=64)
+            live["xw", b, c] = grouped
+            banks = []
+            for m in range(BLOCKS):
+                bank = psum_xw.tile([P, PACK, P], F32, name="xw_ps", tag="bank")
+                banks.append(bank)
                 for j in range(PACK):
-                    g = c * PACK + j
                     nc.tensor.matmul_mx(
                         out=bank[:, j, :],
-                        lhsT=xc[b][:, g * P : (g + 1) * P].bitcast(FP8X4),
-                        lhsT_scale=xs[b][:, g * P : (g + 1) * P],
-                        rhs=wc[:, ob * P : (ob + 1) * P].bitcast(FP8X4),
-                        rhs_scale=ws[:, ob * P : (ob + 1) * P],
+                        lhsT=x_codes[b][:, block(c * PACK + j)].bitcast(FP8X4),
+                        lhsT_scale=x_scales[b][:, block(c * PACK + j)],
+                        rhs=w_codes[:, block(m)].bitcast(FP8X4),
+                        rhs_scale=w_scales[:, block(m)],
                         start=True,
                         stop=True,
                     )
-            elif kind == "E1":
-                b, c, ob = step[1], step[2], step[3]
-                if ("xwg", b, c) not in live:
-                    live[("xwg", b, c)] = xwgp.tile([P, O, PACK], BF16, name="xwg", tag="xwg", align_bytes=64)
-                dst = live[("xwg", b, c)][:, ob * P : (ob + 1) * P, :]
-                src = live[("m1", b, c, ob)][:].rearrange("p j o -> p o j")
-                if step[4] == "V":
-                    nc.vector.tensor_copy(out=dst, in_=src)
-                else:
-                    nc.scalar.copy(out=dst, in_=src)
-            elif kind == "QY":
-                b, c = step[1], step[2]
-                nc.vector.quantize_mx(
-                    out=xwc[b][:, c, :].bitcast(FP8X4),
-                    scales=xws[b][:, c, :],
-                    in_=live[("xwg", b, c)][:].rearrange("p o j -> p (o j)"),
+            for m in range(BLOCKS):
+                copy(engines[m], grouped[:, block(m), :], banks[m][:].rearrange("p j o -> p o j"))
+
+        def xw_quantise(b, c):
+            quantise(xw_codes[b][:, c, :], xw_scales[b][:, c, :], live["xw", b, c][:])
+
+        def degree_matmuls():
+            live["deg"] = psum_out.tile([P, P], F32, name="deg_ps", tag="bank")
+            for k in range(TILES):
+                for g in range(TILES):
+                    nc.tensor.matmul(
+                        live["deg"][:],
+                        lhsT=e_raw[:, k, block(g)],
+                        rhs=select[:, g, :],
+                        start=(k == 0 and g == 0),
+                        stop=(k == TILES - 1 and g == TILES - 1),
+                    )
+
+        def inverse_sqrt_degrees():
+            deg = live["deg"][:, 0:TILES]
+            nc.vector.tensor_scalar(out=deg_floor[:], in0=deg, scalar1=DEG_FLOOR, scalar2=None, op0=ALU.max)
+            nc.scalar.activation(out=deg_sqrt[:], in_=deg_floor[:], func=ACT.Sqrt)
+            nc.vector.reciprocal(out=deg_rsqrt[:], in_=deg_sqrt[:])
+            nc.vector.scalar_tensor_tensor(
+                out=dinv_col[:], in0=deg, scalar=0.0, in1=deg_rsqrt[:], op0=ALU.is_gt, op1=ALU.mult
+            )
+
+        def dinv_spread(h):
+            live["dinv", h] = psum_out.tile([P, H], F32, name="dinv_ps", tag="bank")
+            for q in range(H // P):
+                g = h * (H // P) + q
+                nc.tensor.transpose(
+                    live["dinv", h][:, block(q)], dinv_col[:, g : g + 1].to_broadcast([P, P]), ident[:]
                 )
-            elif kind == "M2":
-                b, m, h = step[1], step[2], step[3]
-                acc = ps2.tile([P, H], F32, name="acc", tag="m2")
-                live[("m2", b, m, h)] = acc
-                for c in range(NC):
+
+        def dinv_copy(h, engine):
+            copy(engine, dinv_row[:, half(h)], live["dinv", h][:])
+
+        def wn_scale(h, c):
+            planes = wn_pool.tile([P, PACK, H], BF16, name="wn_planes", tag="wn_planes")
+            live["planes", h, c] = planes
+            for j in range(PACK):
+                g = c * PACK + j
+                nc.vector.scalar_tensor_tensor(
+                    out=planes[:, j, :],
+                    in0=e_raw[:, g, half(h)],
+                    scalar=dinv_col[:, g : g + 1],
+                    in1=dinv_row[:, half(h)],
+                    op0=ALU.mult,
+                    op1=ALU.mult,
+                )
+
+        def wn_regroup(h, c):
+            live["wn", h, c] = wn_pool.tile([P, H, PACK], BF16, name="wn_grouped", tag="wn_grouped", align_bytes=64)
+            regroup("V", live["wn", h, c][:], live["planes", h, c][:])
+
+        def wn_scale_rows(h, c):
+            planes = wn_pool.tile([P, PACK, H], F32, name="wn_rows", tag="wn_rows", bufs=1)
+            live["planes", h, c] = planes
+            for j in range(PACK):
+                g = c * PACK + j
+                nc.scalar.activation(
+                    out=planes[:, j, :], in_=e_raw[:, g, half(h)], func=ACT.Copy, scale=dinv_col[:, g : g + 1]
+                )
+
+        def wn_scale_columns(h, c):
+            live["wn", h, c] = wn_pool.tile([P, H, PACK], BF16, name="wn_grouped", tag="wn_grouped", align_bytes=64)
+            nc.vector.tensor_tensor(
+                out=live["wn", h, c][:],
+                in0=live["planes", h, c][:].rearrange("p j d -> p d j"),
+                in1=dinv_row[:, half(h)].unsqueeze(2).to_broadcast([P, H, PACK]),
+                op=ALU.mult,
+            )
+
+        def wn_quantise(h, c):
+            quantise(wn_codes[:, c, half(h)], wn_scales[:, c, half(h)], live["wn", h, c][:])
+
+        def second_matmul(b, h, engines):
+            for m in range(BLOCKS):
+                acc = psum_out.tile([P, H], F32, name="out_ps", tag="bank")
+                for c in range(PASSES):
                     nc.tensor.matmul_mx(
                         out=acc[:],
-                        lhsT=xwc[b][:, c, m * P : (m + 1) * P].bitcast(FP8X4),
-                        lhsT_scale=xws[b][:, c, m * P : (m + 1) * P],
-                        rhs=wnc[:, c, h * H : (h + 1) * H].bitcast(FP8X4),
-                        rhs_scale=wns[:, c, h * H : (h + 1) * H],
+                        lhsT=xw_codes[b][:, c, block(m)].bitcast(FP8X4),
+                        lhsT_scale=xw_scales[b][:, c, block(m)],
+                        rhs=wn_codes[:, c, half(h)].bitcast(FP8X4),
+                        rhs_scale=wn_scales[:, c, half(h)],
                         start=(c == 0),
-                        stop=(c == NC - 1),
+                        stop=(c == PASSES - 1),
                     )
-            elif kind == "E2":
-                b, m, h = step[1], step[2], step[3]
-                ost = ostp.tile([P, H], F32, name="ost", tag="ost")
-                if step[4] == "V":
+                result = out_pool.tile([P, H], F32, name="result", tag="result")
+                if engines[m] == "V":
                     nc.vector.tensor_scalar(
-                        out=ost[:],
-                        in0=live[("m2", b, m, h)][:],
-                        scalar1=bias_col[:, m : m + 1],
-                        scalar2=None,
-                        op0=ALU.add,
+                        out=result[:], in0=acc[:], scalar1=bias_col[:, m : m + 1], scalar2=None, op0=ALU.add
                     )
                 else:
                     nc.scalar.activation(
-                        out=ost[:],
-                        in_=live[("m2", b, m, h)][:],
-                        func=ACT.Identity,
-                        bias=bias_col[:, m : m + 1],
-                        scale=1.0,
+                        out=result[:], in_=acc[:], func=ACT.Identity, bias=bias_col[:, m : m + 1], scale=1.0
                     )
-                nc.sync.dma_start(out=out[b, m * P : (m + 1) * P, h * H : (h + 1) * H], in_=ost[:])
+                nc.sync.dma_start(out=out[b, block(m), half(h)], in_=result[:])
+
+        bias_transpose()
+        weight_quantise()
+        x_regroup(0, 0, "V")
+        x_regroup(0, 1, "S")
+        x_quantise(0, 0)
+        bias_copy()
+        first_matmul(0, 0, "SSSS")
+        x_regroup(1, 0, "V")
+        x_quantise(0, 1)
+        first_matmul(0, 1, "SSSS")
+        x_regroup(1, 1, "V")
+        x_quantise(1, 0)
+        x_quantise(1, 1)
+        x_regroup(2, 0, "V")
+        x_regroup(2, 1, "S")
+        xw_quantise(0, 0)
+        xw_quantise(0, 1)
+        x_quantise(2, 0)
+        x_quantise(2, 1)
+        degree_matmuls()
+        inverse_sqrt_degrees()
+        first_matmul(1, 0, "SSSS")
+        dinv_spread(0)
+        dinv_spread(1)
+        dinv_copy(0, "V")
+        first_matmul(1, 1, "SSSS")
+        dinv_copy(1, "S")
+        first_matmul(2, 0, "SSSS")
+        first_matmul(2, 1, "SSSS")
+        wn_scale(0, 0)
+        wn_scale(0, 1)
+        wn_regroup(0, 0)
+        wn_regroup(0, 1)
+        wn_quantise(0, 0)
+        wn_quantise(0, 1)
+        for b in (1, 2):
+            xw_quantise(b, 0)
+            xw_quantise(b, 1)
+        wn_scale_rows(1, 0)
+        for b in (0, 1, 2):
+            second_matmul(b, 0, "SSSS")
+        wn_scale(1, 1)
+        wn_scale_columns(1, 0)
+        wn_regroup(1, 1)
+        wn_quantise(1, 0)
+        wn_quantise(1, 1)
+        for h in range(HALVES):
+            x_regroup(3, h, "V")
+            x_quantise(3, h)
+        for c in range(PASSES):
+            second_matmul(c, 1, "SSSS")
+            first_matmul(3, c, "SVSV")
+            xw_quantise(3, c)
+        second_matmul(2, 1, "SSSS")
+        for h in range(HALVES):
+            second_matmul(3, h, "SVSV")

@@ -38,9 +38,6 @@ def tile_graphembedding_pa_kernel(tc, x, edge_w, weight, bias, out):
         psum_out = ctx.enter_context(tc.psum_pool(name="psum_out", bufs=4))
         ctx.enter_context(tc.manual_schedule())
 
-        bias_rows = const.tile([P, P], BF16, name="bias_rows")
-        nc.gpsimd.memset(bias_rows[:], 0.0)
-        nc.gpsimd.dma_start(out=bias_rows[0:BLOCKS, :], in_=bias.rearrange("(m p) -> m p", p=P))
         ident_bf = const.tile([P, P], BF16, name="ident_bf")
         make_identity(nc, ident_bf[:])
         ident = const.tile([P, P], F32, name="ident")
@@ -50,6 +47,8 @@ def tile_graphembedding_pa_kernel(tc, x, edge_w, weight, bias, out):
         nc.vector.memset(one_col[:], 1.0)
         warm = const.tile([P, 1], F32, name="warm")
         nc.scalar.activation(out=warm[:], in_=one_col[:], func=ACT.Sqrt)
+        bias_rows = const.tile([P, P], BF16, name="bias_rows")
+        nc.vector.memset(bias_rows[:], 0.0)
         select = const.tile([P, TILES, P], BF16, name="select")
         nc.vector.memset(select[:], 0.0)
         for g in range(TILES):
@@ -70,6 +69,7 @@ def tile_graphembedding_pa_kernel(tc, x, edge_w, weight, bias, out):
         for g in range(0, TILES, 2):
             nc.sync.dma_start(out=e_raw[:, g : g + 2, :], in_=e_view[:, g : g + 2, :])
         load_x(3)
+        nc.sync.dma_start(out=bias_rows[0:BLOCKS, :], in_=bias.rearrange("(m p) -> m p", p=P))
 
         w_grouped = keep.tile([P, O, PACK], BF16, name="w_grouped", align_bytes=64)
         w_codes = keep.tile([P, O], U32, name="w_codes", align_bytes=64)
@@ -225,19 +225,30 @@ def tile_graphembedding_pa_kernel(tc, x, edge_w, weight, bias, out):
         def wn_quantise(h, c):
             quantise(wn_codes[:, c, half(h)], wn_scales[:, c, half(h)], live["wn", h, c][:])
 
+        def second_matmul_pass(acc, b, h, m, c):
+            nc.tensor.matmul_mx(
+                out=acc[:],
+                lhsT=xw_codes[b][:, c, block(m)].bitcast(FP8X4),
+                lhsT_scale=xw_scales[b][:, c, block(m)],
+                rhs=wn_codes[:, c, half(h)].bitcast(FP8X4),
+                rhs_scale=wn_scales[:, c, half(h)],
+                start=(c == 0),
+                stop=(c == PASSES - 1),
+            )
+
+        def second_matmul_open(b, h):
+            for m in range(BLOCKS):
+                live["acc", b, h, m] = psum_out.tile([P, H], F32, name="out_ps", tag="bank")
+                second_matmul_pass(live["acc", b, h, m], b, h, m, 0)
+
         def second_matmul(b, h, engines):
             for m in range(BLOCKS):
-                acc = psum_out.tile([P, H], F32, name="out_ps", tag="bank")
-                for c in range(PASSES):
-                    nc.tensor.matmul_mx(
-                        out=acc[:],
-                        lhsT=xw_codes[b][:, c, block(m)].bitcast(FP8X4),
-                        lhsT_scale=xw_scales[b][:, c, block(m)],
-                        rhs=wn_codes[:, c, half(h)].bitcast(FP8X4),
-                        rhs_scale=wn_scales[:, c, half(h)],
-                        start=(c == 0),
-                        stop=(c == PASSES - 1),
-                    )
+                if ("acc", b, h, m) in live:
+                    acc = live["acc", b, h, m]
+                else:
+                    acc = psum_out.tile([P, H], F32, name="out_ps", tag="bank")
+                    second_matmul_pass(acc, b, h, m, 0)
+                second_matmul_pass(acc, b, h, m, 1)
                 result = out_pool.tile([P, H], F32, name="result", tag="result")
                 if engines[m] == "V":
                     nc.vector.tensor_scalar(
@@ -249,12 +260,10 @@ def tile_graphembedding_pa_kernel(tc, x, edge_w, weight, bias, out):
                     )
                 nc.sync.dma_start(out=out[b, block(m), half(h)], in_=result[:])
 
-        bias_transpose()
         weight_quantise()
         x_regroup(0, 0, "V")
         x_regroup(0, 1, "S")
         x_quantise(0, 0)
-        bias_copy()
         first_matmul(0, 0, "SSSS")
         x_regroup(1, 0, "V")
         x_quantise(0, 1)
@@ -278,22 +287,25 @@ def tile_graphembedding_pa_kernel(tc, x, edge_w, weight, bias, out):
         dinv_copy(1, "S")
         first_matmul(2, 0, "SSSS")
         first_matmul(2, 1, "SSSS")
+        bias_transpose()
         wn_scale(0, 0)
         wn_scale(0, 1)
         wn_regroup(0, 0)
         wn_regroup(0, 1)
         wn_quantise(0, 0)
         wn_quantise(0, 1)
+        bias_copy()
         for b in (1, 2):
             xw_quantise(b, 0)
             xw_quantise(b, 1)
         wn_scale_rows(1, 0)
         for b in (0, 1, 2):
             second_matmul(b, 0, "SSSS")
-        wn_scale(1, 1)
         wn_scale_columns(1, 0)
-        wn_regroup(1, 1)
+        wn_scale(1, 1)
         wn_quantise(1, 0)
+        second_matmul_open(0, 1)
+        wn_regroup(1, 1)
         wn_quantise(1, 1)
         for h in range(HALVES):
             x_regroup(3, h, "V")

@@ -20,7 +20,7 @@ PASSES = N // (P * PACK)
 BLOCKS = O // P
 HALVES = 2
 H = N // HALVES
-DEG_FLOOR = 2.0 ** -116
+SQRT_FLOOR = 2.0 ** -58
 
 FLOPS = 2 * N * B * T * O + 2 * N * N * B * O
 
@@ -85,7 +85,7 @@ def tile_graphembedding_pa_kernel(tc, x, edge_w, weight, bias, out):
         deg_sqrt = const.tile([P, TILES], F32, name="deg_sqrt")
         deg_rsqrt = const.tile([P, TILES], F32, name="deg_rsqrt")
         dinv_col = const.tile([P, TILES], F32, name="dinv_col")
-        dinv_row = keep.tile([P, N], F32, name="dinv_row")
+        dinv_row = keep.tile([P, H], F32, name="dinv_row")
         live = {}
 
         def half(h):
@@ -168,9 +168,9 @@ def tile_graphembedding_pa_kernel(tc, x, edge_w, weight, bias, out):
 
         def inverse_sqrt_degrees():
             deg = live["deg"][:, 0:TILES]
-            nc.vector.tensor_scalar(out=deg_floor[:], in0=deg, scalar1=DEG_FLOOR, scalar2=None, op0=ALU.max)
-            nc.scalar.activation(out=deg_sqrt[:], in_=deg_floor[:], func=ACT.Sqrt)
-            nc.vector.reciprocal(out=deg_rsqrt[:], in_=deg_sqrt[:])
+            nc.scalar.activation(out=deg_sqrt[:], in_=deg, func=ACT.Sqrt)
+            nc.vector.tensor_scalar(out=deg_floor[:], in0=deg_sqrt[:], scalar1=SQRT_FLOOR, scalar2=None, op0=ALU.max)
+            nc.vector.reciprocal(out=deg_rsqrt[:], in_=deg_floor[:])
             nc.vector.scalar_tensor_tensor(
                 out=dinv_col[:], in0=deg, scalar=0.0, in1=deg_rsqrt[:], op0=ALU.is_gt, op1=ALU.mult
             )
@@ -183,8 +183,9 @@ def tile_graphembedding_pa_kernel(tc, x, edge_w, weight, bias, out):
                     live["dinv", h][:, block(q)], dinv_col[:, g : g + 1].to_broadcast([P, P]), ident[:]
                 )
 
-        def dinv_copy(h, engine):
-            copy(engine, dinv_row[:, half(h)], live["dinv", h][:])
+        def dinv_copy(h):
+            nc.scalar.copy(out=dinv_row[:], in_=live["dinv", h][:])
+            live["dinv", h] = dinv_row
 
         def wn_scale(h, c):
             planes = wn_pool.tile([P, PACK, H], BF16, name="wn_planes", tag="wn_planes")
@@ -195,7 +196,7 @@ def tile_graphembedding_pa_kernel(tc, x, edge_w, weight, bias, out):
                     out=planes[:, j, :],
                     in0=e_raw[:, g, half(h)],
                     scalar=dinv_col[:, g : g + 1],
-                    in1=dinv_row[:, half(h)],
+                    in1=live["dinv", h][:],
                     op0=ALU.mult,
                     op1=ALU.mult,
                 )
@@ -218,7 +219,7 @@ def tile_graphembedding_pa_kernel(tc, x, edge_w, weight, bias, out):
             nc.vector.tensor_tensor(
                 out=live["wn", h, c][:],
                 in0=live["planes", h, c][:].rearrange("p j d -> p d j"),
-                in1=dinv_row[:, half(h)].unsqueeze(2).to_broadcast([P, H, PACK]),
+                in1=live["dinv", h][:].unsqueeze(2).to_broadcast([P, H, PACK]),
                 op=ALU.mult,
             )
 
@@ -282,9 +283,8 @@ def tile_graphembedding_pa_kernel(tc, x, edge_w, weight, bias, out):
         first_matmul(1, 0, "SSSS")
         dinv_spread(0)
         dinv_spread(1)
-        dinv_copy(0, "V")
         first_matmul(1, 1, "SSSS")
-        dinv_copy(1, "S")
+        dinv_copy(1)
         first_matmul(2, 0, "SSSS")
         first_matmul(2, 1, "SSSS")
         bias_transpose()
@@ -311,9 +311,9 @@ def tile_graphembedding_pa_kernel(tc, x, edge_w, weight, bias, out):
             x_regroup(3, h, "V")
             x_quantise(3, h)
         for c in range(PASSES):
-            second_matmul(c, 1, "SSSS")
+            second_matmul(c, 1, "SSSV")
             first_matmul(3, c, "SVSV")
             xw_quantise(3, c)
-        second_matmul(2, 1, "SSSS")
+        second_matmul(2, 1, "SSSV")
         for h in range(HALVES):
             second_matmul(3, h, "SVSV")

@@ -85,7 +85,6 @@ def tile_graphembedding_pa_kernel(tc, x, edge_w, weight, bias, out):
         deg_sqrt = const.tile([P, TILES], F32, name="deg_sqrt")
         deg_rsqrt = const.tile([P, TILES], F32, name="deg_rsqrt")
         dinv_col = const.tile([P, TILES], F32, name="dinv_col")
-        dinv_row = keep.tile([P, H], F32, name="dinv_row")
         live = {}
 
         def half(h):
@@ -182,10 +181,6 @@ def tile_graphembedding_pa_kernel(tc, x, edge_w, weight, bias, out):
                 nc.tensor.transpose(
                     live["dinv", h][:, block(q)], dinv_col[:, g : g + 1].to_broadcast([P, P]), ident[:]
                 )
-
-        def dinv_copy(h):
-            nc.scalar.copy(out=dinv_row[:], in_=live["dinv", h][:])
-            live["dinv", h] = dinv_row
 
         def wn_scale(h, c):
             planes = wn_pool.tile([P, PACK, H], BF16, name="wn_planes", tag="wn_planes")
@@ -284,7 +279,6 @@ def tile_graphembedding_pa_kernel(tc, x, edge_w, weight, bias, out):
         dinv_spread(0)
         dinv_spread(1)
         first_matmul(1, 1, "SSSS")
-        dinv_copy(1)
         first_matmul(2, 0, "SSSS")
         first_matmul(2, 1, "SSSS")
         bias_transpose()
@@ -310,8 +304,9 @@ def tile_graphembedding_pa_kernel(tc, x, edge_w, weight, bias, out):
         for h in range(HALVES):
             x_regroup(3, h, "V")
             x_quantise(3, h)
+        second_matmul(0, 1, "SSSS")
+        second_matmul(1, 1, "SSSV")
         for c in range(PASSES):
-            second_matmul(c, 1, "SSSV")
             first_matmul(3, c, "SVSV")
             xw_quantise(3, c)
         second_matmul(2, 1, "SSSV")

@@ -15,12 +15,12 @@ P = 128
 PACK = 4
 B, T, N = 4, 512, 1024
 O = T
-TILES = N // P
+NODE_CHUNKS = N // P
+FEATURE_CHUNKS = O // P
 PASSES = N // (P * PACK)
-BLOCKS = O // P
-HALVES = 2
-H = N // HALVES
-SQRT_FLOOR = 2.0 ** -58
+HALF = 512
+HALVES = N // HALF
+ROOT_FLOOR = 2.0 ** -58
 
 FLOPS = 2 * N * B * T * O + 2 * N * N * B * O
 
@@ -38,25 +38,26 @@ def tile_graphembedding_pa_kernel(tc, x, edge_w, weight, bias, out):
         psum_out = ctx.enter_context(tc.psum_pool(name="psum_out", bufs=4))
         ctx.enter_context(tc.manual_schedule())
 
-        ident_bf = const.tile([P, P], BF16, name="ident_bf")
-        make_identity(nc, ident_bf[:])
-        ident = const.tile([P, P], F32, name="ident")
-        make_identity(nc, ident[:])
+        ident_bf16 = const.tile([P, P], BF16, name="ident_bf16")
+        make_identity(nc, ident_bf16[:])
+        ident_f32 = const.tile([P, P], F32, name="ident_f32")
+        make_identity(nc, ident_f32[:])
 
-        one_col = const.tile([P, 1], F32, name="one_col")
-        nc.vector.memset(one_col[:], 1.0)
-        warm = const.tile([P, 1], F32, name="warm")
-        nc.scalar.activation(out=warm[:], in_=one_col[:], func=ACT.Sqrt)
+        one = const.tile([P, 1], F32, name="one")
+        nc.vector.memset(one[:], 1.0)
+        sqrt_of_one = const.tile([P, 1], F32, name="sqrt_of_one")
+        nc.scalar.activation(out=sqrt_of_one[:], in_=one[:], func=ACT.Sqrt)
+
         bias_rows = const.tile([P, P], BF16, name="bias_rows")
         nc.vector.memset(bias_rows[:], 0.0)
-        select = const.tile([P, TILES, P], BF16, name="select")
-        nc.vector.memset(select[:], 0.0)
-        for g in range(TILES):
-            nc.vector.memset(select[:, g, g : g + 1], 1.0)
+        column_g = const.tile([P, NODE_CHUNKS, P], BF16, name="column_g")
+        nc.vector.memset(column_g[:], 0.0)
+        for g in range(NODE_CHUNKS):
+            nc.vector.memset(column_g[:, g, g : g + 1], 1.0)
 
         w_raw = keep.tile([P, PACK, O], BF16, name="w_raw")
         x_raw = [keep.tile([P, PACK, N], BF16, name="x_raw%d" % b) for b in range(B)]
-        e_raw = keep.tile([P, TILES, N], BF16, name="e_raw")
+        e_raw = keep.tile([P, NODE_CHUNKS, N], BF16, name="e_raw")
         e_view = edge_w.rearrange("(g p) d -> p g d", p=P)
 
         def load_x(b):
@@ -66,31 +67,31 @@ def tile_graphembedding_pa_kernel(tc, x, edge_w, weight, bias, out):
         load_x(0)
         load_x(1)
         load_x(2)
-        for g in range(0, TILES, 2):
+        for g in range(0, NODE_CHUNKS, 2):
             nc.sync.dma_start(out=e_raw[:, g : g + 2, :], in_=e_view[:, g : g + 2, :])
         load_x(3)
-        nc.sync.dma_start(out=bias_rows[0:BLOCKS, :], in_=bias.rearrange("(m p) -> m p", p=P))
+        nc.sync.dma_start(out=bias_rows[0:FEATURE_CHUNKS, :], in_=bias.rearrange("(m p) -> m p", p=P))
 
         w_grouped = keep.tile([P, O, PACK], BF16, name="w_grouped", align_bytes=64)
-        w_codes = keep.tile([P, O], U32, name="w_codes", align_bytes=64)
+        w_words = keep.tile([P, O], U32, name="w_words", align_bytes=64)
         w_scales = keep.tile([P, O], U8, name="w_scales", align_bytes=64)
-        x_codes = [keep.tile([P, N], U32, name="x_codes%d" % b, align_bytes=64) for b in range(B)]
+        x_words = [keep.tile([P, N], U32, name="x_words%d" % b, align_bytes=64) for b in range(B)]
         x_scales = [keep.tile([P, N], U8, name="x_scales%d" % b, align_bytes=64) for b in range(B)]
-        xw_codes = [keep.tile([P, PASSES, O], U32, name="xw_codes%d" % b, align_bytes=64) for b in range(B)]
+        xw_words = [keep.tile([P, PASSES, O], U32, name="xw_words%d" % b, align_bytes=64) for b in range(B)]
         xw_scales = [keep.tile([P, PASSES, O], U8, name="xw_scales%d" % b, align_bytes=64) for b in range(B)]
-        wn_codes = keep.tile([P, PASSES, N], U32, name="wn_codes", align_bytes=64)
+        wn_words = keep.tile([P, PASSES, N], U32, name="wn_words", align_bytes=64)
         wn_scales = keep.tile([P, PASSES, N], U8, name="wn_scales", align_bytes=64)
-        bias_col = const.tile([P, BLOCKS], F32, name="bias_col")
-        deg_floor = const.tile([P, TILES], F32, name="deg_floor")
-        deg_sqrt = const.tile([P, TILES], F32, name="deg_sqrt")
-        deg_rsqrt = const.tile([P, TILES], F32, name="deg_rsqrt")
-        dinv_col = const.tile([P, TILES], F32, name="dinv_col")
-        live = {}
+        bias_col = const.tile([P, FEATURE_CHUNKS], F32, name="bias_col")
+        deg_root_floored = const.tile([P, NODE_CHUNKS], F32, name="deg_root_floored")
+        deg_root = const.tile([P, NODE_CHUNKS], F32, name="deg_root")
+        deg_root_inverse = const.tile([P, NODE_CHUNKS], F32, name="deg_root_inverse")
+        dinv_col = const.tile([P, NODE_CHUNKS], F32, name="dinv_col")
+        handed_on = {}
 
-        def half(h):
-            return slice(h * H, (h + 1) * H)
+        def half(i):
+            return slice(i * HALF, (i + 1) * HALF)
 
-        def block(i):
+        def chunk(i):
             return slice(i * P, (i + 1) * P)
 
         def copy(engine, dst, src):
@@ -102,107 +103,104 @@ def tile_graphembedding_pa_kernel(tc, x, edge_w, weight, bias, out):
         def regroup(engine, dst, src):
             copy(
                 engine,
-                dst.rearrange("p (c i) t -> p c t i", i=4),
-                src.rearrange("p t (c i) -> p c t i", i=4),
+                dst.rearrange("p (v i) j -> p v j i", i=4),
+                src.rearrange("p j (v i) -> p v j i", i=4),
             )
 
-        def quantise(codes, scales, grouped):
+        def quantise(words, scales, grouped):
             nc.vector.quantize_mx(
-                out=codes.bitcast(FP8X4), scales=scales, in_=grouped.rearrange("p w j -> p (w j)")
+                out=words.bitcast(FP8X4), scales=scales, in_=grouped.rearrange("p w j -> p (w j)")
             )
 
-        def bias_transpose():
-            live["bias"] = psum_out.tile([P, P], BF16, name="bias_ps", tag="bank")
-            nc.tensor.transpose(live["bias"][:], bias_rows[:], ident_bf[:])
-
-        def bias_copy():
-            nc.vector.tensor_copy(out=bias_col[:], in_=live["bias"][:, 0:BLOCKS])
 
         def weight_quantise():
             regroup("V", w_grouped[:], w_raw[:])
-            quantise(w_codes[:], w_scales[:], w_grouped[:])
+            quantise(w_words[:], w_scales[:], w_grouped[:])
 
-        def x_regroup(b, h, engine):
-            if h == 0:
-                live["x", b] = x_pool.tile([P, N, PACK], BF16, name="x_grouped", tag="x_grouped", align_bytes=64)
-            regroup(engine, live["x", b][:, half(h), :], x_raw[b][:, :, half(h)])
+        def x_regroup(b, c, engine):
+            if c == 0:
+                handed_on["x", b] = x_pool.tile([P, N, PACK], BF16, name="x_grouped", align_bytes=64)
+            regroup(engine, handed_on["x", b][:, half(c), :], x_raw[b][:, :, half(c)])
 
-        def x_quantise(b, h):
-            quantise(x_codes[b][:, half(h)], x_scales[b][:, half(h)], live["x", b][:, half(h), :])
+        def x_quantise(b, c):
+            quantise(x_words[b][:, half(c)], x_scales[b][:, half(c)], handed_on["x", b][:, half(c), :])
 
         def first_matmul(b, c, engines):
-            grouped = xw_pool.tile([P, O, PACK], BF16, name="xw_grouped", tag="xw_grouped", align_bytes=64)
-            live["xw", b, c] = grouped
+            grouped = xw_pool.tile([P, O, PACK], BF16, name="xw_grouped", align_bytes=64)
+            handed_on["xw", b, c] = grouped
             banks = []
-            for m in range(BLOCKS):
-                bank = psum_xw.tile([P, PACK, P], F32, name="xw_ps", tag="bank")
+            for m in range(FEATURE_CHUNKS):
+                bank = psum_xw.tile([P, PACK, P], F32, name="xw_bank")
                 banks.append(bank)
                 for j in range(PACK):
                     nc.tensor.matmul_mx(
                         out=bank[:, j, :],
-                        lhsT=x_codes[b][:, block(c * PACK + j)].bitcast(FP8X4),
-                        lhsT_scale=x_scales[b][:, block(c * PACK + j)],
-                        rhs=w_codes[:, block(m)].bitcast(FP8X4),
-                        rhs_scale=w_scales[:, block(m)],
+                        lhsT=x_words[b][:, chunk(c * PACK + j)].bitcast(FP8X4),
+                        lhsT_scale=x_scales[b][:, chunk(c * PACK + j)],
+                        rhs=w_words[:, chunk(m)].bitcast(FP8X4),
+                        rhs_scale=w_scales[:, chunk(m)],
                         start=True,
                         stop=True,
                     )
-            for m in range(BLOCKS):
-                copy(engines[m], grouped[:, block(m), :], banks[m][:].rearrange("p j o -> p o j"))
+            for m in range(FEATURE_CHUNKS):
+                copy(engines[m], grouped[:, chunk(m), :], banks[m][:].rearrange("p j o -> p o j"))
 
         def xw_quantise(b, c):
-            quantise(xw_codes[b][:, c, :], xw_scales[b][:, c, :], live["xw", b, c][:])
+            quantise(xw_words[b][:, c, :], xw_scales[b][:, c, :], handed_on["xw", b, c][:])
 
-        def degree_matmuls():
-            live["deg"] = psum_out.tile([P, P], F32, name="deg_ps", tag="bank")
-            for k in range(TILES):
-                for g in range(TILES):
+        def degree_sums():
+            handed_on["deg"] = psum_out.tile([P, P], F32, name="deg_bank", tag="bank")
+            for k in range(NODE_CHUNKS):
+                for g in range(NODE_CHUNKS):
                     nc.tensor.matmul(
-                        live["deg"][:],
-                        lhsT=e_raw[:, k, block(g)],
-                        rhs=select[:, g, :],
+                        handed_on["deg"][:],
+                        lhsT=e_raw[:, k, chunk(g)],
+                        rhs=column_g[:, g, :],
                         start=(k == 0 and g == 0),
-                        stop=(k == TILES - 1 and g == TILES - 1),
+                        stop=(k == NODE_CHUNKS - 1 and g == NODE_CHUNKS - 1),
                     )
 
-        def inverse_sqrt_degrees():
-            deg = live["deg"][:, 0:TILES]
-            nc.scalar.activation(out=deg_sqrt[:], in_=deg, func=ACT.Sqrt)
-            nc.vector.tensor_scalar(out=deg_floor[:], in0=deg_sqrt[:], scalar1=SQRT_FLOOR, scalar2=None, op0=ALU.max)
-            nc.vector.reciprocal(out=deg_rsqrt[:], in_=deg_floor[:])
+        def inverse_root_of_degrees():
+            deg = handed_on["deg"][:, 0:NODE_CHUNKS]
+            nc.scalar.activation(out=deg_root[:], in_=deg, func=ACT.Sqrt)
+            nc.vector.tensor_scalar(
+                out=deg_root_floored[:], in0=deg_root[:], scalar1=ROOT_FLOOR, scalar2=None, op0=ALU.max
+            )
+            nc.vector.reciprocal(out=deg_root_inverse[:], in_=deg_root_floored[:])
             nc.vector.scalar_tensor_tensor(
-                out=dinv_col[:], in0=deg, scalar=0.0, in1=deg_rsqrt[:], op0=ALU.is_gt, op1=ALU.mult
+                out=dinv_col[:], in0=deg, scalar=0.0, in1=deg_root_inverse[:], op0=ALU.is_gt, op1=ALU.mult
             )
 
-        def dinv_spread(h):
-            live["dinv", h] = psum_out.tile([P, H], F32, name="dinv_ps", tag="bank")
-            for q in range(H // P):
-                g = h * (H // P) + q
+        def dinv_along_free_axis(h):
+            handed_on["dinv", h] = psum_out.tile([P, HALF], F32, name="dinv_bank", tag="bank")
+            for q in range(HALF // P):
+                g = h * (HALF // P) + q
                 nc.tensor.transpose(
-                    live["dinv", h][:, block(q)], dinv_col[:, g : g + 1].to_broadcast([P, P]), ident[:]
+                    handed_on["dinv", h][:, chunk(q)], dinv_col[:, g : g + 1].to_broadcast([P, P]), ident_f32[:]
                 )
 
+
         def wn_scale(h, c):
-            planes = wn_pool.tile([P, PACK, H], BF16, name="wn_planes", tag="wn_planes")
-            live["planes", h, c] = planes
+            planes = wn_pool.tile([P, PACK, HALF], BF16, name="wn_planes")
+            handed_on["planes", h, c] = planes
             for j in range(PACK):
                 g = c * PACK + j
                 nc.vector.scalar_tensor_tensor(
                     out=planes[:, j, :],
                     in0=e_raw[:, g, half(h)],
                     scalar=dinv_col[:, g : g + 1],
-                    in1=live["dinv", h][:],
+                    in1=handed_on["dinv", h][:],
                     op0=ALU.mult,
                     op1=ALU.mult,
                 )
 
         def wn_regroup(h, c):
-            live["wn", h, c] = wn_pool.tile([P, H, PACK], BF16, name="wn_grouped", tag="wn_grouped", align_bytes=64)
-            regroup("V", live["wn", h, c][:], live["planes", h, c][:])
+            handed_on["wn", h, c] = wn_pool.tile([P, HALF, PACK], BF16, name="wn_grouped", align_bytes=64)
+            regroup("V", handed_on["wn", h, c][:], handed_on["planes", h, c][:])
 
         def wn_scale_rows(h, c):
-            planes = wn_pool.tile([P, PACK, H], F32, name="wn_rows", tag="wn_rows", bufs=1)
-            live["planes", h, c] = planes
+            planes = wn_pool.tile([P, PACK, HALF], F32, name="wn_rows", bufs=1)
+            handed_on["planes", h, c] = planes
             for j in range(PACK):
                 g = c * PACK + j
                 nc.scalar.activation(
@@ -210,51 +208,59 @@ def tile_graphembedding_pa_kernel(tc, x, edge_w, weight, bias, out):
                 )
 
         def wn_scale_columns(h, c):
-            live["wn", h, c] = wn_pool.tile([P, H, PACK], BF16, name="wn_grouped", tag="wn_grouped", align_bytes=64)
+            handed_on["wn", h, c] = wn_pool.tile([P, HALF, PACK], BF16, name="wn_grouped", align_bytes=64)
             nc.vector.tensor_tensor(
-                out=live["wn", h, c][:],
-                in0=live["planes", h, c][:].rearrange("p j d -> p d j"),
-                in1=live["dinv", h][:].unsqueeze(2).to_broadcast([P, H, PACK]),
+                out=handed_on["wn", h, c][:],
+                in0=handed_on["planes", h, c][:].rearrange("p j d -> p d j"),
+                in1=handed_on["dinv", h][:].unsqueeze(2).to_broadcast([P, HALF, PACK]),
                 op=ALU.mult,
             )
 
         def wn_quantise(h, c):
-            quantise(wn_codes[:, c, half(h)], wn_scales[:, c, half(h)], live["wn", h, c][:])
+            quantise(wn_words[:, c, half(h)], wn_scales[:, c, half(h)], handed_on["wn", h, c][:])
 
-        def second_matmul_pass(acc, b, h, m, c):
+        def bias_transpose():
+            handed_on["bias"] = psum_out.tile([P, P], BF16, name="bias_bank", tag="bank")
+            nc.tensor.transpose(handed_on["bias"][:], bias_rows[:], ident_bf16[:])
+
+        def bias_copy():
+            nc.vector.tensor_copy(out=bias_col[:], in_=handed_on["bias"][:, 0:FEATURE_CHUNKS])
+
+        def second_matmul_pass(bank, b, h, m, c):
             nc.tensor.matmul_mx(
-                out=acc[:],
-                lhsT=xw_codes[b][:, c, block(m)].bitcast(FP8X4),
-                lhsT_scale=xw_scales[b][:, c, block(m)],
-                rhs=wn_codes[:, c, half(h)].bitcast(FP8X4),
+                out=bank[:],
+                lhsT=xw_words[b][:, c, chunk(m)].bitcast(FP8X4),
+                lhsT_scale=xw_scales[b][:, c, chunk(m)],
+                rhs=wn_words[:, c, half(h)].bitcast(FP8X4),
                 rhs_scale=wn_scales[:, c, half(h)],
                 start=(c == 0),
                 stop=(c == PASSES - 1),
             )
 
-        def second_matmul_open(b, h):
-            for m in range(BLOCKS):
-                live["acc", b, h, m] = psum_out.tile([P, H], F32, name="out_ps", tag="bank")
-                second_matmul_pass(live["acc", b, h, m], b, h, m, 0)
+        def second_matmul_first_passes(b, h):
+            for m in range(FEATURE_CHUNKS):
+                handed_on["out", b, h, m] = psum_out.tile([P, HALF], F32, name="out_bank", tag="bank")
+                second_matmul_pass(handed_on["out", b, h, m], b, h, m, 0)
 
         def second_matmul(b, h, engines):
-            for m in range(BLOCKS):
-                if ("acc", b, h, m) in live:
-                    acc = live["acc", b, h, m]
+            for m in range(FEATURE_CHUNKS):
+                if ("out", b, h, m) in handed_on:
+                    bank = handed_on["out", b, h, m]
                 else:
-                    acc = psum_out.tile([P, H], F32, name="out_ps", tag="bank")
-                    second_matmul_pass(acc, b, h, m, 0)
-                second_matmul_pass(acc, b, h, m, 1)
-                result = out_pool.tile([P, H], F32, name="result", tag="result")
+                    bank = psum_out.tile([P, HALF], F32, name="out_bank", tag="bank")
+                    second_matmul_pass(bank, b, h, m, 0)
+                second_matmul_pass(bank, b, h, m, 1)
+                result = out_pool.tile([P, HALF], F32, name="result")
                 if engines[m] == "V":
                     nc.vector.tensor_scalar(
-                        out=result[:], in0=acc[:], scalar1=bias_col[:, m : m + 1], scalar2=None, op0=ALU.add
+                        out=result[:], in0=bank[:], scalar1=bias_col[:, m : m + 1], scalar2=None, op0=ALU.add
                     )
                 else:
                     nc.scalar.activation(
-                        out=result[:], in_=acc[:], func=ACT.Identity, bias=bias_col[:, m : m + 1], scale=1.0
+                        out=result[:], in_=bank[:], func=ACT.Identity, bias=bias_col[:, m : m + 1], scale=1.0
                     )
-                nc.sync.dma_start(out=out[b, block(m), half(h)], in_=result[:])
+                nc.sync.dma_start(out=out[b, chunk(m), half(h)], in_=result[:])
+
 
         weight_quantise()
         x_regroup(0, 0, "V")
@@ -273,15 +279,17 @@ def tile_graphembedding_pa_kernel(tc, x, edge_w, weight, bias, out):
         xw_quantise(0, 1)
         x_quantise(2, 0)
         x_quantise(2, 1)
-        degree_matmuls()
-        inverse_sqrt_degrees()
+
+        degree_sums()
+        inverse_root_of_degrees()
         first_matmul(1, 0, "SSSS")
-        dinv_spread(0)
-        dinv_spread(1)
+        dinv_along_free_axis(0)
+        dinv_along_free_axis(1)
         first_matmul(1, 1, "SSSS")
         first_matmul(2, 0, "SSSS")
         first_matmul(2, 1, "SSSS")
         bias_transpose()
+
         wn_scale(0, 0)
         wn_scale(0, 1)
         wn_regroup(0, 0)
@@ -292,18 +300,20 @@ def tile_graphembedding_pa_kernel(tc, x, edge_w, weight, bias, out):
         for b in (1, 2):
             xw_quantise(b, 0)
             xw_quantise(b, 1)
+
         wn_scale_rows(1, 0)
         for b in (0, 1, 2):
             second_matmul(b, 0, "SSSS")
         wn_scale_columns(1, 0)
         wn_scale(1, 1)
         wn_quantise(1, 0)
-        second_matmul_open(0, 1)
+        second_matmul_first_passes(0, 1)
         wn_regroup(1, 1)
         wn_quantise(1, 1)
-        for h in range(HALVES):
-            x_regroup(3, h, "V")
-            x_quantise(3, h)
+
+        for c in range(PASSES):
+            x_regroup(3, c, "V")
+            x_quantise(3, c)
         second_matmul(0, 1, "SSSS")
         second_matmul(1, 1, "SSSV")
         for c in range(PASSES):

@@ -20,6 +20,7 @@ FEATURE_CHUNKS = O // P
 PASSES = N // (P * PACK)
 HALF = 512
 HALVES = N // HALF
+DEG_COLUMNS = 32
 ROOT_FLOOR = 2.0 ** -58
 
 FLOPS = 2 * N * B * T * O + 2 * N * N * B * O
@@ -50,18 +51,24 @@ def tile_graphembedding_pa_kernel(tc, x, edge_w, weight, bias, out):
 
         bias_rows = const.tile([P, P], BF16, name="bias_rows")
         nc.vector.memset(bias_rows[:], 0.0)
-        column_g = const.tile([P, NODE_CHUNKS, P], BF16, name="column_g")
+        column_g = const.tile([P, NODE_CHUNKS, DEG_COLUMNS], BF16, name="column_g")
         nc.vector.memset(column_g[:], 0.0)
         for g in range(NODE_CHUNKS):
             nc.vector.memset(column_g[:, g, g : g + 1], 1.0)
 
         w_raw = keep.tile([P, PACK, O], BF16, name="w_raw")
-        x_raw = [keep.tile([P, PACK, N], BF16, name="x_raw%d" % b) for b in range(B)]
+        x_raw = {
+            (b, c): keep.tile([P, PACK, HALF], BF16, name="x_raw%d%d" % (b, c))
+            for b in range(B)
+            for c in range(PASSES)
+        }
         e_raw = keep.tile([P, NODE_CHUNKS, N], BF16, name="e_raw")
         e_view = edge_w.rearrange("(g p) d -> p g d", p=P)
 
         def load_x(b):
-            nc.sync.dma_start(out=x_raw[b][:], in_=x[b].rearrange("(p j) s -> p j s", j=PACK))
+            x_view = x[b].rearrange("(p j) s -> p j s", j=PACK)
+            for c in range(PASSES):
+                nc.sync.dma_start(out=x_raw[b, c][:], in_=x_view[:, :, c * HALF : (c + 1) * HALF])
 
         nc.sync.dma_start(out=w_raw[:], in_=weight.rearrange("(p j) o -> p j o", j=PACK))
         load_x(0)
@@ -113,14 +120,20 @@ def tile_graphembedding_pa_kernel(tc, x, edge_w, weight, bias, out):
             )
 
 
+        def weight_regroup():
+            for engine, features in (("V", slice(0, O // 2)), ("S", slice(O // 2, O))):
+                regroup(engine, w_grouped[:, features, :], w_raw[:, :, features])
+
         def weight_quantise():
-            regroup("V", w_grouped[:], w_raw[:])
             quantise(w_words[:], w_scales[:], w_grouped[:])
 
-        def x_regroup(b, c, engine):
+        def x_regroup(b, c, engines):
             if c == 0:
                 handed_on["x", b] = x_pool.tile([P, N, PACK], BF16, name="x_grouped", align_bytes=64)
-            regroup(engine, handed_on["x", b][:, half(c), :], x_raw[b][:, :, half(c)])
+            width = HALF // len(engines)
+            for i, engine in enumerate(engines):
+                nodes = slice(i * width, (i + 1) * width)
+                regroup(engine, handed_on["x", b][:, half(c), :][:, nodes, :], x_raw[b, c][:, :, nodes])
 
         def x_quantise(b, c):
             quantise(x_words[b][:, half(c)], x_scales[b][:, half(c)], handed_on["x", b][:, half(c), :])
@@ -149,7 +162,7 @@ def tile_graphembedding_pa_kernel(tc, x, edge_w, weight, bias, out):
             quantise(xw_words[b][:, c, :], xw_scales[b][:, c, :], handed_on["xw", b, c][:])
 
         def degree_sums():
-            handed_on["deg"] = psum_out.tile([P, P], F32, name="deg_bank", tag="bank")
+            handed_on["deg"] = psum_out.tile([P, DEG_COLUMNS], F32, name="deg_bank", tag="bank")
             for k in range(NODE_CHUNKS):
                 for g in range(NODE_CHUNKS):
                     nc.tensor.matmul(
@@ -262,13 +275,14 @@ def tile_graphembedding_pa_kernel(tc, x, edge_w, weight, bias, out):
                 nc.sync.dma_start(out=out[b, chunk(m), half(h)], in_=result[:])
 
 
+        weight_regroup()
+        x_regroup(0, 0, "VS")
         weight_quantise()
-        x_regroup(0, 0, "V")
-        x_regroup(0, 1, "S")
         x_quantise(0, 0)
+        x_regroup(0, 1, "VS")
         first_matmul(0, 0, "SSSS")
-        x_regroup(1, 0, "V")
         x_quantise(0, 1)
+        x_regroup(1, 0, "V")
         first_matmul(0, 1, "SSSS")
         x_regroup(1, 1, "V")
         x_quantise(1, 0)

@@ -34,9 +34,9 @@ def tile_graphembedding_pa_kernel(tc, x, edge_w, weight, bias, out):
         x_pool = ctx.enter_context(tc.tile_pool(name="x_pool", bufs=2))
         xw_pool = ctx.enter_context(tc.tile_pool(name="xw_pool", bufs=6))
         wn_pool = ctx.enter_context(tc.tile_pool(name="wn_pool", bufs=2))
-        out_pool = ctx.enter_context(tc.tile_pool(name="out_pool", bufs=8))
-        psum_xw = ctx.enter_context(tc.psum_pool(name="psum_xw", bufs=4))
-        psum_out = ctx.enter_context(tc.psum_pool(name="psum_out", bufs=4))
+        out_pool = ctx.enter_context(tc.tile_pool(name="out_pool", bufs=12))
+        psum_xw = ctx.enter_context(tc.psum_pool(name="psum_xw", bufs=3))
+        psum_out = ctx.enter_context(tc.psum_pool(name="psum_out", bufs=5))
         ctx.enter_context(tc.manual_schedule())
 
         ident_bf16 = const.tile([P, P], BF16, name="ident_bf16")
@@ -57,25 +57,33 @@ def tile_graphembedding_pa_kernel(tc, x, edge_w, weight, bias, out):
             nc.vector.memset(column_g[:, g, g : g + 1], 1.0)
 
         w_raw = keep.tile([P, PACK, O], BF16, name="w_raw")
-        x_raw = {
-            (b, c): keep.tile([P, PACK, HALF], BF16, name="x_raw%d%d" % (b, c))
-            for b in range(B)
-            for c in range(PASSES)
-        }
+        x_raw = {(0, c): keep.tile([P, PACK, HALF], BF16, name="x_raw0%d" % c) for c in range(PASSES)}
+        x_whole = {b: keep.tile([P, PACK, N], BF16, name="x_raw%d" % b) for b in range(1, B)}
+        for b in range(1, B):
+            for c in range(PASSES):
+                x_raw[b, c] = x_whole[b][:, :, c * HALF : (c + 1) * HALF]
         e_raw = keep.tile([P, NODE_CHUNKS, N], BF16, name="e_raw")
         e_view = edge_w.rearrange("(g p) d -> p g d", p=P)
 
         def load_x(b):
             x_view = x[b].rearrange("(p j) s -> p j s", j=PACK)
-            for c in range(PASSES):
-                nc.sync.dma_start(out=x_raw[b, c][:], in_=x_view[:, :, c * HALF : (c + 1) * HALF])
+            if b == 0:
+                for c in range(PASSES):
+                    nc.sync.dma_start(out=x_raw[b, c][:], in_=x_view[:, :, c * HALF : (c + 1) * HALF])
+            else:
+                nc.sync.dma_start(out=x_whole[b][:], in_=x_view)
+
+        def load_edges(first, end):
+            nc.sync.dma_start(out=e_raw[:, first:end, :], in_=e_view[:, first:end, :])
 
         nc.sync.dma_start(out=w_raw[:], in_=weight.rearrange("(p j) o -> p j o", j=PACK))
         load_x(0)
         load_x(1)
+        load_edges(0, 2)
+        load_edges(2, 4)
         load_x(2)
-        for g in range(0, NODE_CHUNKS, 2):
-            nc.sync.dma_start(out=e_raw[:, g : g + 2, :], in_=e_view[:, g : g + 2, :])
+        load_edges(4, 6)
+        load_edges(6, 8)
         load_x(3)
         nc.sync.dma_start(out=bias_rows[0:FEATURE_CHUNKS, :], in_=bias.rearrange("(m p) -> m p", p=P))
 
@@ -138,13 +146,10 @@ def tile_graphembedding_pa_kernel(tc, x, edge_w, weight, bias, out):
         def x_quantise(b, c):
             quantise(x_words[b][:, half(c)], x_scales[b][:, half(c)], handed_on["x", b][:, half(c), :])
 
-        def first_matmul(b, c, engines):
-            grouped = xw_pool.tile([P, O, PACK], BF16, name="xw_grouped", align_bytes=64)
-            handed_on["xw", b, c] = grouped
-            banks = []
+        def first_matmul(b, c):
             for m in range(FEATURE_CHUNKS):
                 bank = psum_xw.tile([P, PACK, P], F32, name="xw_bank")
-                banks.append(bank)
+                handed_on["xw_bank", b, c, m] = bank
                 for j in range(PACK):
                     nc.tensor.matmul_mx(
                         out=bank[:, j, :],
@@ -155,15 +160,21 @@ def tile_graphembedding_pa_kernel(tc, x, edge_w, weight, bias, out):
                         start=True,
                         stop=True,
                     )
-            for m in range(FEATURE_CHUNKS):
-                copy(engines[m], grouped[:, chunk(m), :], banks[m][:].rearrange("p j o -> p o j"))
+
+        def xw_copy(b, c, engines, first=0):
+            if first == 0:
+                handed_on["xw", b, c] = xw_pool.tile([P, O, PACK], BF16, name="xw_grouped", align_bytes=64)
+            for m, engine in enumerate(engines, first):
+                bank = handed_on["xw_bank", b, c, m]
+                copy(engine, handed_on["xw", b, c][:, chunk(m), :], bank[:].rearrange("p j o -> p o j"))
 
         def xw_quantise(b, c):
             quantise(xw_words[b][:, c, :], xw_scales[b][:, c, :], handed_on["xw", b, c][:])
 
-        def degree_sums():
-            handed_on["deg"] = psum_out.tile([P, DEG_COLUMNS], F32, name="deg_bank", tag="bank")
-            for k in range(NODE_CHUNKS):
+        def degree_sums(source_chunks):
+            if source_chunks[0] == 0:
+                handed_on["deg"] = psum_out.tile([P, DEG_COLUMNS], F32, name="deg_bank", tag="bank")
+            for k in source_chunks:
                 for g in range(NODE_CHUNKS):
                     nc.tensor.matmul(
                         handed_on["deg"][:],
@@ -193,38 +204,30 @@ def tile_graphembedding_pa_kernel(tc, x, edge_w, weight, bias, out):
                 )
 
 
-        def wn_scale(h, c):
-            planes = wn_pool.tile([P, PACK, HALF], BF16, name="wn_planes")
-            handed_on["planes", h, c] = planes
-            for j in range(PACK):
+        def wn_scale_rows(h, c, engines):
+            rows = wn_pool.tile([P, PACK, HALF], F32, name="wn_rows", bufs=4)
+            handed_on["rows", h, c] = rows
+            for j, engine in enumerate(engines):
                 g = c * PACK + j
-                nc.vector.scalar_tensor_tensor(
-                    out=planes[:, j, :],
-                    in0=e_raw[:, g, half(h)],
-                    scalar=dinv_col[:, g : g + 1],
-                    in1=handed_on["dinv", h][:],
-                    op0=ALU.mult,
-                    op1=ALU.mult,
-                )
-
-        def wn_regroup(h, c):
-            handed_on["wn", h, c] = wn_pool.tile([P, HALF, PACK], BF16, name="wn_grouped", align_bytes=64)
-            regroup("V", handed_on["wn", h, c][:], handed_on["planes", h, c][:])
-
-        def wn_scale_rows(h, c):
-            planes = wn_pool.tile([P, PACK, HALF], F32, name="wn_rows", bufs=1)
-            handed_on["planes", h, c] = planes
-            for j in range(PACK):
-                g = c * PACK + j
-                nc.scalar.activation(
-                    out=planes[:, j, :], in_=e_raw[:, g, half(h)], func=ACT.Copy, scale=dinv_col[:, g : g + 1]
-                )
+                if engine == "G":
+                    nc.gpsimd.tensor_scalar(
+                        out=rows[:, j, :],
+                        in0=e_raw[:, g, half(h)],
+                        scalar1=dinv_col[:, g : g + 1],
+                        scalar2=0.0,
+                        op0=ALU.mult,
+                        op1=ALU.add,
+                    )
+                else:
+                    nc.scalar.activation(
+                        out=rows[:, j, :], in_=e_raw[:, g, half(h)], func=ACT.Copy, scale=dinv_col[:, g : g + 1]
+                    )
 
         def wn_scale_columns(h, c):
             handed_on["wn", h, c] = wn_pool.tile([P, HALF, PACK], BF16, name="wn_grouped", align_bytes=64)
             nc.vector.tensor_tensor(
                 out=handed_on["wn", h, c][:],
-                in0=handed_on["planes", h, c][:].rearrange("p j d -> p d j"),
+                in0=handed_on["rows", h, c][:].rearrange("p j d -> p d j"),
                 in1=handed_on["dinv", h][:].unsqueeze(2).to_broadcast([P, HALF, PACK]),
                 op=ALU.mult,
             )
@@ -250,19 +253,11 @@ def tile_graphembedding_pa_kernel(tc, x, edge_w, weight, bias, out):
                 stop=(c == PASSES - 1),
             )
 
-        def second_matmul_first_passes(b, h):
-            for m in range(FEATURE_CHUNKS):
-                handed_on["out", b, h, m] = psum_out.tile([P, HALF], F32, name="out_bank", tag="bank")
-                second_matmul_pass(handed_on["out", b, h, m], b, h, m, 0)
-
         def second_matmul(b, h, engines):
             for m in range(FEATURE_CHUNKS):
-                if ("out", b, h, m) in handed_on:
-                    bank = handed_on["out", b, h, m]
-                else:
-                    bank = psum_out.tile([P, HALF], F32, name="out_bank", tag="bank")
-                    second_matmul_pass(bank, b, h, m, 0)
-                second_matmul_pass(bank, b, h, m, 1)
+                bank = psum_out.tile([P, HALF], F32, name="out_bank", tag="bank")
+                for c in range(PASSES):
+                    second_matmul_pass(bank, b, h, m, c)
                 result = out_pool.tile([P, HALF], F32, name="result")
                 if engines[m] == "V":
                     nc.vector.tensor_scalar(
@@ -280,58 +275,66 @@ def tile_graphembedding_pa_kernel(tc, x, edge_w, weight, bias, out):
         weight_quantise()
         x_quantise(0, 0)
         x_regroup(0, 1, "VS")
-        first_matmul(0, 0, "SSSS")
+        first_matmul(0, 0)
+        xw_copy(0, 0, "SSSS")
         x_quantise(0, 1)
+        first_matmul(0, 1)
+        xw_copy(0, 1, "SSSS")
         x_regroup(1, 0, "V")
-        first_matmul(0, 1, "SSSS")
         x_regroup(1, 1, "V")
         x_quantise(1, 0)
         x_quantise(1, 1)
-        x_regroup(2, 0, "V")
-        x_regroup(2, 1, "S")
+        degree_sums(range(0, 4))
+        first_matmul(1, 0)
+        xw_copy(1, 0, "SSSS")
         xw_quantise(0, 0)
         xw_quantise(0, 1)
-        x_quantise(2, 0)
-        x_quantise(2, 1)
-
-        degree_sums()
+        x_regroup(2, 0, "V")
+        x_regroup(2, 1, "V")
+        xw_quantise(1, 0)
+        degree_sums(range(4, 8))
         inverse_root_of_degrees()
-        first_matmul(1, 0, "SSSS")
         dinv_along_free_axis(0)
         dinv_along_free_axis(1)
-        first_matmul(1, 1, "SSSS")
-        first_matmul(2, 0, "SSSS")
-        first_matmul(2, 1, "SSSS")
-        bias_transpose()
+        first_matmul(1, 1)
 
-        wn_scale(0, 0)
-        wn_scale(0, 1)
-        wn_regroup(0, 0)
-        wn_regroup(0, 1)
+        wn_scale_rows(0, 0, "SSSG")
+        wn_scale_rows(0, 1, "GGGG")
+        wn_scale_rows(1, 0, "GGGG")
+        xw_copy(1, 1, "SSSS")
+        x_quantise(2, 0)
+        x_quantise(2, 1)
+        first_matmul(2, 0)
+        xw_copy(2, 0, "SSSS")
+        wn_scale_columns(0, 0)
+        xw_quantise(1, 1)
+        wn_scale_rows(1, 1, "GGGG")
+        wn_scale_columns(0, 1)
+        first_matmul(2, 1)
+        xw_copy(2, 1, "SSSS")
+        bias_transpose()
         wn_quantise(0, 0)
         wn_quantise(0, 1)
         bias_copy()
-        for b in (1, 2):
-            xw_quantise(b, 0)
-            xw_quantise(b, 1)
 
-        wn_scale_rows(1, 0)
+        wn_scale_columns(1, 0)
+        xw_quantise(2, 0)
+        xw_quantise(2, 1)
+        wn_scale_columns(1, 1)
+        wn_quantise(1, 0)
+        wn_quantise(1, 1)
         for b in (0, 1, 2):
             second_matmul(b, 0, "SSSS")
-        wn_scale_columns(1, 0)
-        wn_scale(1, 1)
-        wn_quantise(1, 0)
-        second_matmul_first_passes(0, 1)
-        wn_regroup(1, 1)
-        wn_quantise(1, 1)
+        x_regroup(3, 0, "V")
+        x_regroup(3, 1, "V")
+        x_quantise(3, 0)
+        x_quantise(3, 1)
 
-        for c in range(PASSES):
-            x_regroup(3, c, "V")
-            x_quantise(3, c)
         second_matmul(0, 1, "SSSS")
-        second_matmul(1, 1, "SSSV")
+        second_matmul(1, 1, "SSSS")
         for c in range(PASSES):
-            first_matmul(3, c, "SVSV")
+            first_matmul(3, c)
+            xw_copy(3, c, "SVSV")
             xw_quantise(3, c)
         second_matmul(2, 1, "SSSV")
         for h in range(HALVES):

@@ -225,10 +225,11 @@ def tile_graphembedding_pa_kernel(tc, x, edge_w, weight, bias, out):
 
         def wn_scale_columns(h, c):
             handed_on["wn", h, c] = wn_pool.tile([P, HALF, PACK], BF16, name="wn_grouped", align_bytes=64)
+            dinv_runs = handed_on["dinv", h][:].rearrange("p (v i) -> p v i", i=4)
             nc.vector.tensor_tensor(
-                out=handed_on["wn", h, c][:],
-                in0=handed_on["rows", h, c][:].rearrange("p j d -> p d j"),
-                in1=handed_on["dinv", h][:].unsqueeze(2).to_broadcast([P, HALF, PACK]),
+                out=handed_on["wn", h, c][:].rearrange("p (v i) j -> p v j i", i=4),
+                in0=handed_on["rows", h, c][:].rearrange("p j (v i) -> p v j i", i=4),
+                in1=dinv_runs.unsqueeze(2).to_broadcast([P, HALF // 4, PACK, 4]),
                 op=ALU.mult,
             )
 

@@ -101,6 +101,7 @@ def tile_graphembedding_pa_kernel(tc, x, edge_w, weight, bias, out):
         deg_root = const.tile([P, NODE_CHUNKS], F32, name="deg_root")
         deg_root_inverse = const.tile([P, NODE_CHUNKS], F32, name="deg_root_inverse")
         dinv_col = const.tile([P, NODE_CHUNKS], F32, name="dinv_col")
+        dinv_late = [const.tile([P, NODE_CHUNKS], F32, name="dinv_late%d" % i) for i in range(HALVES)]
         handed_on = {}
 
         def half(i):
@@ -204,7 +205,7 @@ def tile_graphembedding_pa_kernel(tc, x, edge_w, weight, bias, out):
                 )
 
 
-        def wn_scale_rows(h, c, engines):
+        def wn_scale_rows(h, c, engines, dinv=dinv_col):
             rows = wn_pool.tile([P, PACK, HALF], F32, name="wn_rows", bufs=4)
             handed_on["rows", h, c] = rows
             for j, engine in enumerate(engines):
@@ -213,14 +214,22 @@ def tile_graphembedding_pa_kernel(tc, x, edge_w, weight, bias, out):
                     nc.gpsimd.tensor_scalar(
                         out=rows[:, j, :],
                         in0=e_raw[:, g, half(h)],
-                        scalar1=dinv_col[:, g : g + 1],
+                        scalar1=dinv[:, g : g + 1],
                         scalar2=0.0,
                         op0=ALU.mult,
                         op1=ALU.add,
                     )
+                elif engine == "V":
+                    nc.vector.tensor_scalar(
+                        out=rows[:, j, :],
+                        in0=e_raw[:, g, half(h)],
+                        scalar1=dinv[:, g : g + 1],
+                        scalar2=None,
+                        op0=ALU.mult,
+                    )
                 else:
                     nc.scalar.activation(
-                        out=rows[:, j, :], in_=e_raw[:, g, half(h)], func=ACT.Copy, scale=dinv_col[:, g : g + 1]
+                        out=rows[:, j, :], in_=e_raw[:, g, half(h)], func=ACT.Copy, scale=dinv[:, g : g + 1]
                     )
 
         def wn_scale_columns(h, c):
@@ -254,13 +263,13 @@ def tile_graphembedding_pa_kernel(tc, x, edge_w, weight, bias, out):
                 stop=(c == PASSES - 1),
             )
 
-        def second_matmul(b, h, engines):
-            for m in range(FEATURE_CHUNKS):
+        def second_matmul(b, h, engines, first=0):
+            for m, engine in enumerate(engines, first):
                 bank = psum_out.tile([P, HALF], F32, name="out_bank", tag="bank")
                 for c in range(PASSES):
                     second_matmul_pass(bank, b, h, m, c)
                 result = out_pool.tile([P, HALF], F32, name="result")
-                if engines[m] == "V":
+                if engine == "V":
                     nc.vector.tensor_scalar(
                         out=result[:], in0=bank[:], scalar1=bias_col[:, m : m + 1], scalar2=None, op0=ALU.add
                     )
@@ -291,33 +300,35 @@ def tile_graphembedding_pa_kernel(tc, x, edge_w, weight, bias, out):
         xw_quantise(0, 0)
         xw_quantise(0, 1)
         x_regroup(2, 0, "V")
-        x_regroup(2, 1, "V")
+        x_regroup(2, 1, "VS")
         xw_quantise(1, 0)
         degree_sums(range(4, 8))
         inverse_root_of_degrees()
         dinv_along_free_axis(0)
         dinv_along_free_axis(1)
         first_matmul(1, 1)
+        bias_transpose()
 
-        wn_scale_rows(0, 0, "SSSG")
-        wn_scale_rows(0, 1, "GGGG")
-        wn_scale_rows(1, 0, "GGGG")
+        wn_scale_rows(0, 0, "SSVV")
         xw_copy(1, 1, "SSSS")
         x_quantise(2, 0)
         x_quantise(2, 1)
+        nc.vector.tensor_copy(out=dinv_late[0][:], in_=dinv_col[:])
+        wn_scale_rows(0, 1, "GGVV", dinv=dinv_late[0])
+        wn_scale_rows(1, 0, "GGGG", dinv=dinv_late[0])
         first_matmul(2, 0)
         xw_copy(2, 0, "SSSS")
         wn_scale_columns(0, 0)
-        xw_quantise(1, 1)
-        wn_scale_rows(1, 1, "GGGG")
+        bias_copy()
         wn_scale_columns(0, 1)
         first_matmul(2, 1)
         xw_copy(2, 1, "SSSS")
-        bias_transpose()
         wn_quantise(0, 0)
         wn_quantise(0, 1)
-        bias_copy()
+        xw_quantise(1, 1)
 
+        nc.vector.tensor_copy(out=dinv_late[1][:], in_=dinv_col[:])
+        wn_scale_rows(1, 1, "GGGG", dinv=dinv_late[1])
         wn_scale_columns(1, 0)
         xw_quantise(2, 0)
         xw_quantise(2, 1)
@@ -332,11 +343,15 @@ def tile_graphembedding_pa_kernel(tc, x, edge_w, weight, bias, out):
         x_quantise(3, 1)
 
         second_matmul(0, 1, "SSSS")
-        second_matmul(1, 1, "SSSS")
-        for c in range(PASSES):
-            first_matmul(3, c)
-            xw_copy(3, c, "SVSV")
-            xw_quantise(3, c)
-        second_matmul(2, 1, "SSSV")
+        second_matmul(1, 1, "SS")
+        first_matmul(3, 0)
+        xw_copy(3, 0, "VVVV")
+        second_matmul(1, 1, "SS", first=2)
+        first_matmul(3, 1)
+        xw_copy(3, 1, "V")
+        xw_quantise(3, 0)
+        xw_copy(3, 1, "VVV", first=1)
+        xw_quantise(3, 1)
+        second_matmul(2, 1, "SSSS")
         for h in range(HALVES):
             second_matmul(3, h, "SVSV")

@@ -101,7 +101,6 @@ def tile_graphembedding_pa_kernel(tc, x, edge_w, weight, bias, out):
         deg_root = const.tile([P, NODE_CHUNKS], F32, name="deg_root")
         deg_root_inverse = const.tile([P, NODE_CHUNKS], F32, name="deg_root_inverse")
         dinv_col = const.tile([P, NODE_CHUNKS], F32, name="dinv_col")
-        dinv_late = [const.tile([P, NODE_CHUNKS], F32, name="dinv_late%d" % i) for i in range(HALVES)]
         handed_on = {}
 
         def half(i):
@@ -185,9 +184,11 @@ def tile_graphembedding_pa_kernel(tc, x, edge_w, weight, bias, out):
                         stop=(k == NODE_CHUNKS - 1 and g == NODE_CHUNKS - 1),
                     )
 
+        def root_of_degrees():
+            nc.scalar.activation(out=deg_root[:], in_=handed_on["deg"][:, 0:NODE_CHUNKS], func=ACT.Sqrt)
+
         def inverse_root_of_degrees():
             deg = handed_on["deg"][:, 0:NODE_CHUNKS]
-            nc.scalar.activation(out=deg_root[:], in_=deg, func=ACT.Sqrt)
             nc.vector.tensor_scalar(
                 out=deg_root_floored[:], in0=deg_root[:], scalar1=ROOT_FLOOR, scalar2=None, op0=ALU.max
             )
@@ -205,7 +206,7 @@ def tile_graphembedding_pa_kernel(tc, x, edge_w, weight, bias, out):
                 )
 
 
-        def wn_scale_rows(h, c, engines, dinv=dinv_col):
+        def wn_scale_rows(h, c, engines):
             rows = wn_pool.tile([P, PACK, HALF], F32, name="wn_rows", bufs=4)
             handed_on["rows", h, c] = rows
             for j, engine in enumerate(engines):
@@ -214,7 +215,7 @@ def tile_graphembedding_pa_kernel(tc, x, edge_w, weight, bias, out):
                     nc.gpsimd.tensor_scalar(
                         out=rows[:, j, :],
                         in0=e_raw[:, g, half(h)],
-                        scalar1=dinv[:, g : g + 1],
+                        scalar1=dinv_col[:, g : g + 1],
                         scalar2=0.0,
                         op0=ALU.mult,
                         op1=ALU.add,
@@ -223,13 +224,13 @@ def tile_graphembedding_pa_kernel(tc, x, edge_w, weight, bias, out):
                     nc.vector.tensor_scalar(
                         out=rows[:, j, :],
                         in0=e_raw[:, g, half(h)],
-                        scalar1=dinv[:, g : g + 1],
+                        scalar1=dinv_col[:, g : g + 1],
                         scalar2=None,
                         op0=ALU.mult,
                     )
                 else:
                     nc.scalar.activation(
-                        out=rows[:, j, :], in_=e_raw[:, g, half(h)], func=ACT.Copy, scale=dinv[:, g : g + 1]
+                        out=rows[:, j, :], in_=e_raw[:, g, half(h)], func=ACT.Copy, scale=dinv_col[:, g : g + 1]
                     )
 
         def wn_scale_columns(h, c):
@@ -300,22 +301,23 @@ def tile_graphembedding_pa_kernel(tc, x, edge_w, weight, bias, out):
         xw_quantise(0, 0)
         xw_quantise(0, 1)
         x_regroup(2, 0, "V")
-        x_regroup(2, 1, "VS")
-        xw_quantise(1, 0)
         degree_sums(range(4, 8))
+        root_of_degrees()
+        x_regroup(2, 1, "VS")
         inverse_root_of_degrees()
+        xw_quantise(1, 0)
         dinv_along_free_axis(0)
         dinv_along_free_axis(1)
         first_matmul(1, 1)
         bias_transpose()
 
         wn_scale_rows(0, 0, "SSVV")
+        wn_scale_rows(0, 1, "GGGG")
+        wn_scale_rows(1, 0, "GGGG")
+        wn_scale_rows(1, 1, "GGGG")
         xw_copy(1, 1, "SSSS")
         x_quantise(2, 0)
         x_quantise(2, 1)
-        nc.vector.tensor_copy(out=dinv_late[0][:], in_=dinv_col[:])
-        wn_scale_rows(0, 1, "GGVV", dinv=dinv_late[0])
-        wn_scale_rows(1, 0, "GGGG", dinv=dinv_late[0])
         first_matmul(2, 0)
         xw_copy(2, 0, "SSSS")
         wn_scale_columns(0, 0)
@@ -327,8 +329,6 @@ def tile_graphembedding_pa_kernel(tc, x, edge_w, weight, bias, out):
         wn_quantise(0, 1)
         xw_quantise(1, 1)
 
-        nc.vector.tensor_copy(out=dinv_late[1][:], in_=dinv_col[:])
-        wn_scale_rows(1, 1, "GGGG", dinv=dinv_late[1])
         wn_scale_columns(1, 0)
         xw_quantise(2, 0)
         xw_quantise(2, 1)
@@ -338,19 +338,19 @@ def tile_graphembedding_pa_kernel(tc, x, edge_w, weight, bias, out):
         for b in (0, 1, 2):
             second_matmul(b, 0, "SSSS")
         x_regroup(3, 0, "V")
-        x_regroup(3, 1, "V")
+        x_regroup(3, 1, "VS")
         x_quantise(3, 0)
         x_quantise(3, 1)
 
         second_matmul(0, 1, "SSSS")
         second_matmul(1, 1, "SS")
         first_matmul(3, 0)
-        xw_copy(3, 0, "VVVV")
+        xw_copy(3, 0, "VVVS")
         second_matmul(1, 1, "SS", first=2)
         first_matmul(3, 1)
         xw_copy(3, 1, "V")
         xw_quantise(3, 0)
-        xw_copy(3, 1, "VVV", first=1)
+        xw_copy(3, 1, "VVS", first=1)
         xw_quantise(3, 1)
         second_matmul(2, 1, "SSSS")
         for h in range(HALVES):

@@ -101,6 +101,7 @@ def tile_graphembedding_pa_kernel(tc, x, edge_w, weight, bias, out):
         deg_root = const.tile([P, NODE_CHUNKS], F32, name="deg_root")
         deg_root_inverse = const.tile([P, NODE_CHUNKS], F32, name="deg_root_inverse")
         dinv_col = const.tile([P, NODE_CHUNKS], F32, name="dinv_col")
+        dinv_late = [const.tile([P, NODE_CHUNKS], F32, name="dinv_late%d" % h) for h in range(HALVES)]
         handed_on = {}
 
         def half(i):
@@ -206,16 +207,17 @@ def tile_graphembedding_pa_kernel(tc, x, edge_w, weight, bias, out):
                 )
 
 
-        def wn_scale_rows(h, c, engines):
-            rows = wn_pool.tile([P, PACK, HALF], F32, name="wn_rows", bufs=4)
-            handed_on["rows", h, c] = rows
-            for j, engine in enumerate(engines):
+        def wn_scale_rows(h, c, engines, first=0, dinv=dinv_col):
+            if ("rows", h, c) not in handed_on:
+                handed_on["rows", h, c] = wn_pool.tile([P, PACK, HALF], F32, name="wn_rows", bufs=4)
+            rows = handed_on["rows", h, c]
+            for j, engine in enumerate(engines, first):
                 g = c * PACK + j
                 if engine == "G":
                     nc.gpsimd.tensor_scalar(
                         out=rows[:, j, :],
                         in0=e_raw[:, g, half(h)],
-                        scalar1=dinv_col[:, g : g + 1],
+                        scalar1=dinv[:, g : g + 1],
                         scalar2=0.0,
                         op0=ALU.mult,
                         op1=ALU.add,
@@ -224,14 +226,17 @@ def tile_graphembedding_pa_kernel(tc, x, edge_w, weight, bias, out):
                     nc.vector.tensor_scalar(
                         out=rows[:, j, :],
                         in0=e_raw[:, g, half(h)],
-                        scalar1=dinv_col[:, g : g + 1],
+                        scalar1=dinv[:, g : g + 1],
                         scalar2=None,
                         op0=ALU.mult,
                     )
                 else:
                     nc.scalar.activation(
-                        out=rows[:, j, :], in_=e_raw[:, g, half(h)], func=ACT.Copy, scale=dinv_col[:, g : g + 1]
+                        out=rows[:, j, :], in_=e_raw[:, g, half(h)], func=ACT.Copy, scale=dinv[:, g : g + 1]
                     )
+
+        def let_gpsimd_start(h):
+            nc.vector.tensor_copy(out=dinv_late[h][:], in_=dinv_col[:])
 
         def wn_scale_columns(h, c):
             handed_on["wn", h, c] = wn_pool.tile([P, HALF, PACK], BF16, name="wn_grouped", align_bytes=64)
@@ -304,20 +309,21 @@ def tile_graphembedding_pa_kernel(tc, x, edge_w, weight, bias, out):
         degree_sums(range(4, 8))
         root_of_degrees()
         x_regroup(2, 1, "VS")
-        inverse_root_of_degrees()
         xw_quantise(1, 0)
+        x_quantise(2, 0)
+        inverse_root_of_degrees()
         dinv_along_free_axis(0)
         dinv_along_free_axis(1)
         first_matmul(1, 1)
         bias_transpose()
 
-        wn_scale_rows(0, 0, "SSVV")
-        wn_scale_rows(0, 1, "GGGG")
-        wn_scale_rows(1, 0, "GGGG")
-        wn_scale_rows(1, 1, "GGGG")
+        wn_scale_rows(0, 0, "SSSV")
+        wn_scale_rows(0, 1, "VV", first=2)
         xw_copy(1, 1, "SSSS")
-        x_quantise(2, 0)
         x_quantise(2, 1)
+        let_gpsimd_start(0)
+        wn_scale_rows(0, 1, "GG", dinv=dinv_late[0])
+        wn_scale_rows(1, 0, "GGGG", dinv=dinv_late[0])
         first_matmul(2, 0)
         xw_copy(2, 0, "SSSS")
         wn_scale_columns(0, 0)
@@ -329,16 +335,21 @@ def tile_graphembedding_pa_kernel(tc, x, edge_w, weight, bias, out):
         wn_quantise(0, 1)
         xw_quantise(1, 1)
 
+        let_gpsimd_start(1)
+        wn_scale_rows(1, 1, "GG", dinv=dinv_late[1])
         wn_scale_columns(1, 0)
+        second_matmul(0, 0, "SS")
+        wn_scale_rows(1, 1, "SS", first=2)
+        second_matmul(0, 0, "SS", first=2)
         xw_quantise(2, 0)
         xw_quantise(2, 1)
         wn_scale_columns(1, 1)
         wn_quantise(1, 0)
         wn_quantise(1, 1)
-        for b in (0, 1, 2):
+        for b in (1, 2):
             second_matmul(b, 0, "SSSS")
         x_regroup(3, 0, "V")
-        x_regroup(3, 1, "VS")
+        x_regroup(3, 1, "V")
         x_quantise(3, 0)
         x_quantise(3, 1)
 

@@ -147,8 +147,8 @@ def tile_graphembedding_pa_kernel(tc, x, edge_w, weight, bias, out):
         def x_quantise(b, c):
             quantise(x_words[b][:, half(c)], x_scales[b][:, half(c)], handed_on["x", b][:, half(c), :])
 
-        def first_matmul(b, c):
-            for m in range(FEATURE_CHUNKS):
+        def first_matmul(b, c, features=range(FEATURE_CHUNKS)):
+            for m in features:
                 bank = psum_xw.tile([P, PACK, P], F32, name="xw_bank")
                 handed_on["xw_bank", b, c, m] = bank
                 for j in range(PACK):
@@ -355,14 +355,18 @@ def tile_graphembedding_pa_kernel(tc, x, edge_w, weight, bias, out):
 
         second_matmul(0, 1, "SSSS")
         second_matmul(1, 1, "SS")
-        first_matmul(3, 0)
+        first_matmul(3, 0, (0, 1))
+        second_matmul(1, 1, "S", first=2)
+        first_matmul(3, 0, (2, 3))
         xw_copy(3, 0, "VVVS")
-        second_matmul(1, 1, "SS", first=2)
-        first_matmul(3, 1)
+        second_matmul(1, 1, "S", first=3)
+        first_matmul(3, 1, (0, 1))
+        second_matmul(2, 1, "S")
+        first_matmul(3, 1, (2, 3))
         xw_copy(3, 1, "V")
         xw_quantise(3, 0)
         xw_copy(3, 1, "VVS", first=1)
         xw_quantise(3, 1)
-        second_matmul(2, 1, "SSSS")
+        second_matmul(2, 1, "SSS", first=1)
         for h in range(HALVES):
             second_matmul(3, h, "SVSV")

@@ -317,15 +317,17 @@ def tile_graphembedding_pa_kernel(tc, x, edge_w, weight, bias, out):
         first_matmul(1, 1)
         bias_transpose()
 
-        wn_scale_rows(0, 0, "SSSV")
+        wn_scale_rows(0, 0, "SSS")
         wn_scale_rows(0, 1, "VV", first=2)
         xw_copy(1, 1, "SSSS")
         x_quantise(2, 1)
+        wn_scale_rows(0, 0, "V", first=3)
         let_gpsimd_start(0)
         wn_scale_rows(0, 1, "GG", dinv=dinv_late[0])
         wn_scale_rows(1, 0, "GGGG", dinv=dinv_late[0])
         first_matmul(2, 0)
         xw_copy(2, 0, "SSSS")
+        wn_scale_rows(1, 1, "S", first=2)
         wn_scale_columns(0, 0)
         bias_copy()
         wn_scale_columns(0, 1)
@@ -339,7 +341,7 @@ def tile_graphembedding_pa_kernel(tc, x, edge_w, weight, bias, out):
         wn_scale_rows(1, 1, "GG", dinv=dinv_late[1])
         wn_scale_columns(1, 0)
         second_matmul(0, 0, "SS")
-        wn_scale_rows(1, 1, "SS", first=2)
+        wn_scale_rows(1, 1, "S", first=3)
         second_matmul(0, 0, "SS", first=2)
         xw_quantise(2, 0)
         xw_quantise(2, 1)
@@ -361,11 +363,11 @@ def tile_graphembedding_pa_kernel(tc, x, edge_w, weight, bias, out):
         xw_copy(3, 0, "VVVS")
         second_matmul(1, 1, "S", first=3)
         first_matmul(3, 1, (0, 1))
+        xw_copy(3, 1, "VS")
+        xw_quantise(3, 0)
         second_matmul(2, 1, "S")
         first_matmul(3, 1, (2, 3))
-        xw_copy(3, 1, "V")
-        xw_quantise(3, 0)
-        xw_copy(3, 1, "VVS", first=1)
+        xw_copy(3, 1, "VS", first=2)
         xw_quantise(3, 1)
         second_matmul(2, 1, "SSS", first=1)
         for h in range(HALVES):

from contextlib import ExitStack

import concourse.mybir as mybir
from concourse.masks import make_identity

F32 = mybir.dt.float32
BF16 = mybir.dt.bfloat16
U32 = mybir.dt.uint32
U8 = mybir.dt.uint8
FP8X4 = mybir.dt.float8_e4m3fn_x4
ALU = mybir.AluOpType
ACT = mybir.ActivationFunctionType

P = 128
PACK = 4
B, T, N = 4, 512, 1024
O = T
NODE_CHUNKS = N // P
FEATURE_CHUNKS = O // P
PASSES = N // (P * PACK)
HALF = 512
HALVES = N // HALF
DEG_COLUMNS = 32
ROOT_FLOOR = 2.0 ** -58

FLOPS = 2 * N * B * T * O + 2 * N * N * B * O


def tile_graphembedding_pa_kernel(tc, x, edge_w, weight, bias, out):
    nc = tc.nc
    with ExitStack() as ctx:
        const = ctx.enter_context(tc.tile_pool(name="const", bufs=1))
        keep = ctx.enter_context(tc.tile_pool(name="keep", bufs=1))
        x_pool = ctx.enter_context(tc.tile_pool(name="x_pool", bufs=2))
        xw_pool = ctx.enter_context(tc.tile_pool(name="xw_pool", bufs=6))
        wn_pool = ctx.enter_context(tc.tile_pool(name="wn_pool", bufs=2))
        out_pool = ctx.enter_context(tc.tile_pool(name="out_pool", bufs=12))
        psum_xw = ctx.enter_context(tc.psum_pool(name="psum_xw", bufs=3))
        psum_out = ctx.enter_context(tc.psum_pool(name="psum_out", bufs=5))
        ctx.enter_context(tc.manual_schedule())

        ident_bf16 = const.tile([P, P], BF16, name="ident_bf16")
        make_identity(nc, ident_bf16[:])
        ident_f32 = const.tile([P, P], F32, name="ident_f32")
        make_identity(nc, ident_f32[:])

        one = const.tile([P, 1], F32, name="one")
        nc.vector.memset(one[:], 1.0)
        sqrt_of_one = const.tile([P, 1], F32, name="sqrt_of_one")
        nc.scalar.activation(out=sqrt_of_one[:], in_=one[:], func=ACT.Sqrt)

        bias_rows = const.tile([P, P], BF16, name="bias_rows")
        nc.vector.memset(bias_rows[:], 0.0)
        column_g = const.tile([P, NODE_CHUNKS, DEG_COLUMNS], BF16, name="column_g")
        nc.vector.memset(column_g[:], 0.0)
        for g in range(NODE_CHUNKS):
            nc.vector.memset(column_g[:, g, g : g + 1], 1.0)

        w_raw = keep.tile([P, PACK, O], BF16, name="w_raw")
        x_raw = {(0, c): keep.tile([P, PACK, HALF], BF16, name="x_raw0%d" % c) for c in range(PASSES)}
        x_whole = {b: keep.tile([P, PACK, N], BF16, name="x_raw%d" % b) for b in range(1, B)}
        for b in range(1, B):
            for c in range(PASSES):
                x_raw[b, c] = x_whole[b][:, :, c * HALF : (c + 1) * HALF]
        e_raw = keep.tile([P, NODE_CHUNKS, N], BF16, name="e_raw")
        e_view = edge_w.rearrange("(g p) d -> p g d", p=P)

        def load_x(b):
            x_view = x[b].rearrange("(p j) s -> p j s", j=PACK)
            if b == 0:
                for c in range(PASSES):
                    nc.sync.dma_start(out=x_raw[b, c][:], in_=x_view[:, :, c * HALF : (c + 1) * HALF])
            else:
                nc.sync.dma_start(out=x_whole[b][:], in_=x_view)

        def load_edges(first, end):
            nc.sync.dma_start(out=e_raw[:, first:end, :], in_=e_view[:, first:end, :])

        nc.sync.dma_start(out=w_raw[:], in_=weight.rearrange("(p j) o -> p j o", j=PACK))
        load_x(0)
        load_x(1)
        load_edges(0, 2)
        load_edges(2, 4)
        load_x(2)
        load_edges(4, 6)
        load_edges(6, 8)
        load_x(3)
        nc.sync.dma_start(out=bias_rows[0:FEATURE_CHUNKS, :], in_=bias.rearrange("(m p) -> m p", p=P))

        w_grouped = keep.tile([P, O, PACK], BF16, name="w_grouped", align_bytes=64)
        w_words = keep.tile([P, O], U32, name="w_words", align_bytes=64)
        w_scales = keep.tile([P, O], U8, name="w_scales", align_bytes=64)
        x_words = [keep.tile([P, N], U32, name="x_words%d" % b, align_bytes=64) for b in range(B)]
        x_scales = [keep.tile([P, N], U8, name="x_scales%d" % b, align_bytes=64) for b in range(B)]
        xw_words = [keep.tile([P, PASSES, O], U32, name="xw_words%d" % b, align_bytes=64) for b in range(B)]
        xw_scales = [keep.tile([P, PASSES, O], U8, name="xw_scales%d" % b, align_bytes=64) for b in range(B)]
        wn_words = keep.tile([P, PASSES, N], U32, name="wn_words", align_bytes=64)
        wn_scales = keep.tile([P, PASSES, N], U8, name="wn_scales", align_bytes=64)
        bias_col = const.tile([P, FEATURE_CHUNKS], F32, name="bias_col")
        deg_root_floored = const.tile([P, NODE_CHUNKS], F32, name="deg_root_floored")
        deg_root = const.tile([P, NODE_CHUNKS], F32, name="deg_root")
        deg_root_inverse = const.tile([P, NODE_CHUNKS], F32, name="deg_root_inverse")
        dinv_col = const.tile([P, NODE_CHUNKS], F32, name="dinv_col")
        dinv_late = [const.tile([P, NODE_CHUNKS], F32, name="dinv_late%d" % h) for h in range(HALVES)]
        handed_on = {}

        def half(i):
            return slice(i * HALF, (i + 1) * HALF)

        def chunk(i):
            return slice(i * P, (i + 1) * P)

        def copy(engine, dst, src):
            if engine == "V":
                nc.vector.tensor_copy(out=dst, in_=src)
            else:
                nc.scalar.copy(out=dst, in_=src)

        def regroup(engine, dst, src):
            copy(
                engine,
                dst.rearrange("p (v i) j -> p v j i", i=4),
                src.rearrange("p j (v i) -> p v j i", i=4),
            )

        def quantise(words, scales, grouped):
            nc.vector.quantize_mx(
                out=words.bitcast(FP8X4), scales=scales, in_=grouped.rearrange("p w j -> p (w j)")
            )


        def weight_regroup():
            for engine, features in (("V", slice(0, O // 2)), ("S", slice(O // 2, O))):
                regroup(engine, w_grouped[:, features, :], w_raw[:, :, features])

        def weight_quantise():
            quantise(w_words[:], w_scales[:], w_grouped[:])

        def x_regroup(b, c, engines):
            if c == 0:
                handed_on["x", b] = x_pool.tile([P, N, PACK], BF16, name="x_grouped", align_bytes=64)
            width = HALF // len(engines)
            for i, engine in enumerate(engines):
                nodes = slice(i * width, (i + 1) * width)
                regroup(engine, handed_on["x", b][:, half(c), :][:, nodes, :], x_raw[b, c][:, :, nodes])

        def x_quantise(b, c):
            quantise(x_words[b][:, half(c)], x_scales[b][:, half(c)], handed_on["x", b][:, half(c), :])

        def first_matmul(b, c, features=range(FEATURE_CHUNKS)):
            for m in features:
                bank = psum_xw.tile([P, PACK, P], F32, name="xw_bank")
                handed_on["xw_bank", b, c, m] = bank
                for j in range(PACK):
                    nc.tensor.matmul_mx(
                        out=bank[:, j, :],
                        lhsT=x_words[b][:, chunk(c * PACK + j)].bitcast(FP8X4),
                        lhsT_scale=x_scales[b][:, chunk(c * PACK + j)],
                        rhs=w_words[:, chunk(m)].bitcast(FP8X4),
                        rhs_scale=w_scales[:, chunk(m)],
                        start=True,
                        stop=True,
                    )

        def xw_copy(b, c, engines, first=0):
            if first == 0:
                handed_on["xw", b, c] = xw_pool.tile([P, O, PACK], BF16, name="xw_grouped", align_bytes=64)
            for m, engine in enumerate(engines, first):
                bank = handed_on["xw_bank", b, c, m]
                copy(engine, handed_on["xw", b, c][:, chunk(m), :], bank[:].rearrange("p j o -> p o j"))

        def xw_quantise(b, c):
            quantise(xw_words[b][:, c, :], xw_scales[b][:, c, :], handed_on["xw", b, c][:])

        def degree_sums(source_chunks):
            if source_chunks[0] == 0:
                handed_on["deg"] = psum_out.tile([P, DEG_COLUMNS], F32, name="deg_bank", tag="bank")
            for k in source_chunks:
                for g in range(NODE_CHUNKS):
                    nc.tensor.matmul(
                        handed_on["deg"][:],
                        lhsT=e_raw[:, k, chunk(g)],
                        rhs=column_g[:, g, :],
                        start=(k == 0 and g == 0),
                        stop=(k == NODE_CHUNKS - 1 and g == NODE_CHUNKS - 1),
                    )

        def root_of_degrees():
            nc.scalar.activation(out=deg_root[:], in_=handed_on["deg"][:, 0:NODE_CHUNKS], func=ACT.Sqrt)

        def inverse_root_of_degrees():
            deg = handed_on["deg"][:, 0:NODE_CHUNKS]
            nc.vector.tensor_scalar(
                out=deg_root_floored[:], in0=deg_root[:], scalar1=ROOT_FLOOR, scalar2=None, op0=ALU.max
            )
            nc.vector.reciprocal(out=deg_root_inverse[:], in_=deg_root_floored[:])
            nc.vector.scalar_tensor_tensor(
                out=dinv_col[:], in0=deg, scalar=0.0, in1=deg_root_inverse[:], op0=ALU.is_gt, op1=ALU.mult
            )

        def dinv_along_free_axis(h):
            handed_on["dinv", h] = psum_out.tile([P, HALF], F32, name="dinv_bank", tag="bank")
            for q in range(HALF // P):
                g = h * (HALF // P) + q
                nc.tensor.transpose(
                    handed_on["dinv", h][:, chunk(q)], dinv_col[:, g : g + 1].to_broadcast([P, P]), ident_f32[:]
                )


        def wn_scale_rows(h, c, engines, first=0, dinv=dinv_col):
            if ("rows", h, c) not in handed_on:
                handed_on["rows", h, c] = wn_pool.tile([P, PACK, HALF], F32, name="wn_rows", bufs=4)
            rows = handed_on["rows", h, c]
            for j, engine in enumerate(engines, first):
                g = c * PACK + j
                if engine == "G":
                    nc.gpsimd.tensor_scalar(
                        out=rows[:, j, :],
                        in0=e_raw[:, g, half(h)],
                        scalar1=dinv[:, g : g + 1],
                        scalar2=0.0,
                        op0=ALU.mult,
                        op1=ALU.add,
                    )
                elif engine == "V":
                    nc.vector.tensor_scalar(
                        out=rows[:, j, :],
                        in0=e_raw[:, g, half(h)],
                        scalar1=dinv[:, g : g + 1],
                        scalar2=None,
                        op0=ALU.mult,
                    )
                else:
                    nc.scalar.activation(
                        out=rows[:, j, :], in_=e_raw[:, g, half(h)], func=ACT.Copy, scale=dinv[:, g : g + 1]
                    )

        def let_gpsimd_start(h):
            nc.vector.tensor_copy(out=dinv_late[h][:], in_=dinv_col[:])

        def wn_scale_columns(h, c):
            handed_on["wn", h, c] = wn_pool.tile([P, HALF, PACK], BF16, name="wn_grouped", align_bytes=64)
            dinv_runs = handed_on["dinv", h][:].rearrange("p (v i) -> p v i", i=4)
            nc.vector.tensor_tensor(
                out=handed_on["wn", h, c][:].rearrange("p (v i) j -> p v j i", i=4),
                in0=handed_on["rows", h, c][:].rearrange("p j (v i) -> p v j i", i=4),
                in1=dinv_runs.unsqueeze(2).to_broadcast([P, HALF // 4, PACK, 4]),
                op=ALU.mult,
            )

        def wn_quantise(h, c):
            quantise(wn_words[:, c, half(h)], wn_scales[:, c, half(h)], handed_on["wn", h, c][:])

        def bias_transpose():
            handed_on["bias"] = psum_out.tile([P, P], BF16, name="bias_bank", tag="bank")
            nc.tensor.transpose(handed_on["bias"][:], bias_rows[:], ident_bf16[:])

        def bias_copy():
            nc.vector.tensor_copy(out=bias_col[:], in_=handed_on["bias"][:, 0:FEATURE_CHUNKS])

        def second_matmul_pass(bank, b, h, m, c):
            nc.tensor.matmul_mx(
                out=bank[:],
                lhsT=xw_words[b][:, c, chunk(m)].bitcast(FP8X4),
                lhsT_scale=xw_scales[b][:, c, chunk(m)],
                rhs=wn_words[:, c, half(h)].bitcast(FP8X4),
                rhs_scale=wn_scales[:, c, half(h)],
                start=(c == 0),
                stop=(c == PASSES - 1),
            )

        def second_matmul(b, h, engines, first=0):
            for m, engine in enumerate(engines, first):
                bank = psum_out.tile([P, HALF], F32, name="out_bank", tag="bank")
                for c in range(PASSES):
                    second_matmul_pass(bank, b, h, m, c)
                result = out_pool.tile([P, HALF], F32, name="result")
                if engine == "V":
                    nc.vector.tensor_scalar(
                        out=result[:], in0=bank[:], scalar1=bias_col[:, m : m + 1], scalar2=None, op0=ALU.add
                    )
                else:
                    nc.scalar.activation(
                        out=result[:], in_=bank[:], func=ACT.Identity, bias=bias_col[:, m : m + 1], scale=1.0
                    )
                nc.sync.dma_start(out=out[b, chunk(m), half(h)], in_=result[:])


        weight_regroup()
        x_regroup(0, 0, "VS")
        weight_quantise()
        x_quantise(0, 0)
        x_regroup(0, 1, "VS")
        first_matmul(0, 0)
        xw_copy(0, 0, "SSSS")
        x_quantise(0, 1)
        first_matmul(0, 1)
        xw_copy(0, 1, "SSSS")
        x_regroup(1, 0, "V")
        x_regroup(1, 1, "V")
        x_quantise(1, 0)
        x_quantise(1, 1)
        degree_sums(range(0, 4))
        first_matmul(1, 0)
        xw_copy(1, 0, "SSSS")
        xw_quantise(0, 0)
        xw_quantise(0, 1)
        x_regroup(2, 0, "V")
        degree_sums(range(4, 8))
        root_of_degrees()
        x_regroup(2, 1, "VS")
        xw_quantise(1, 0)
        x_quantise(2, 0)
        inverse_root_of_degrees()
        dinv_along_free_axis(0)
        dinv_along_free_axis(1)
        first_matmul(1, 1)
        bias_transpose()

        wn_scale_rows(0, 0, "SSS")
        wn_scale_rows(0, 1, "VV", first=2)
        xw_copy(1, 1, "SSSS")
        x_quantise(2, 1)
        wn_scale_rows(0, 0, "V", first=3)
        let_gpsimd_start(0)
        wn_scale_rows(0, 1, "GG", dinv=dinv_late[0])
        wn_scale_rows(1, 0, "GGGG", dinv=dinv_late[0])
        first_matmul(2, 0)
        xw_copy(2, 0, "SSSS")
        wn_scale_rows(1, 1, "S", first=2)
        wn_scale_columns(0, 0)
        bias_copy()
        wn_scale_columns(0, 1)
        first_matmul(2, 1)
        xw_copy(2, 1, "SSSS")
        wn_quantise(0, 0)
        wn_quantise(0, 1)
        xw_quantise(1, 1)

        let_gpsimd_start(1)
        wn_scale_rows(1, 1, "GG", dinv=dinv_late[1])
        wn_scale_columns(1, 0)
        second_matmul(0, 0, "SS")
        wn_scale_rows(1, 1, "S", first=3)
        second_matmul(0, 0, "SS", first=2)
        xw_quantise(2, 0)
        xw_quantise(2, 1)
        wn_scale_columns(1, 1)
        wn_quantise(1, 0)
        wn_quantise(1, 1)
        for b in (1, 2):
            second_matmul(b, 0, "SSSS")
        x_regroup(3, 0, "V")
        x_regroup(3, 1, "V")
        x_quantise(3, 0)
        x_quantise(3, 1)

        second_matmul(0, 1, "SSSS")
        second_matmul(1, 1, "SS")
        first_matmul(3, 0, (0, 1))
        second_matmul(1, 1, "S", first=2)
        first_matmul(3, 0, (2, 3))
        xw_copy(3, 0, "VVVS")
        second_matmul(1, 1, "S", first=3)
        first_matmul(3, 1, (0, 1))
        xw_copy(3, 1, "VS")
        xw_quantise(3, 0)
        second_matmul(2, 1, "S")
        first_matmul(3, 1, (2, 3))
        xw_copy(3, 1, "VS", first=2)
        xw_quantise(3, 1)
        second_matmul(2, 1, "SSS", first=1)
        for h in range(HALVES):
            second_matmul(3, h, "SVSV")
